import numpy as np
import ml_dtypes


def mxq(x, axis, fmt="e4m3"):
    dtype, down = {"e4m3": (ml_dtypes.float8_e4m3fn, 7), "e5m2": (ml_dtypes.float8_e5m2, 14)}[fmt]
    v = np.moveaxis(np.asarray(x, np.float32).astype(ml_dtypes.bfloat16).astype(np.float64), axis, -1)
    blocks = v.reshape(v.shape[:-1] + (-1, 32))
    amax = np.abs(blocks).max(-1, keepdims=True)
    byte = np.maximum(np.where(amax > 0, np.frexp(amax)[1] - 1 + 127, 0) - down, 1)
    scale = np.exp2(byte - 127.0)
    codes = (blocks / scale).astype(np.float32).astype(dtype).astype(np.float64)
    return np.moveaxis((codes * scale).reshape(v.shape), -1, axis)


WIDE = False


def mx_kscale(k):
    if not WIDE:
        return np.ones(k)
    levels = np.array([10, -10, 5, -5, 0])
    a = np.random.permutation(np.resize(levels, k // 512 * 4)).reshape(k // 512, 4)
    idx = np.arange(k)
    return np.exp2(a[idx // 512, idx % 128 // 32])


BF16 = ml_dtypes.bfloat16


def bf(x):
    return np.asarray(x, np.float32).astype(BF16)


def f64(x):
    return np.asarray(x).astype(np.float64)


B, S, IN, OUT, Q, NS, R, ALPHA = 8, 1024, 1024, 2048, 4, 8, 128, 1024
DQ = IN // Q


def setup_inputs():
    s = mx_kscale(IN)
    return {"x": bf(np.random.standard_normal((B, S, IN)) * s),
            "weights": bf(np.random.uniform(0.0, 1.0, (B, Q, NS))),
            "lora_a": bf(np.random.standard_normal((Q, NS, DQ, R)) * 1.7 / np.sqrt(NS * IN) / s.reshape(Q, DQ)[:, None, :, None])}


def reference(x, weights, lora_a):
    w, la = f64(weights), f64(lora_a)
    a_mix = sum(w[:, :, k, None, None] * la[None, :, k] for k in range(NS))
    a_mix = a_mix.reshape(B, IN, R)
    return mxq(f64(x), 2, "e4m3") @ mxq(a_mix, 1, "e4m3")

@@ -1,0 +1,246 @@
+from contextlib import ExitStack
+
+import concourse.mybir as mybir
+from concourse.masks import make_identity
+
+F32 = mybir.dt.float32
+BF16 = mybir.dt.bfloat16
+U32 = mybir.dt.uint32
+U8 = mybir.dt.uint8
+FP8X4 = mybir.dt.float8_e4m3fn_x4
+ALU = mybir.AluOpType
+AX = mybir.AxisListType
+
+B, S, IN, Q, NS, R = 8, 1024, 1024, 4, 8, 128
+P = 128
+PACK = 4
+PASSES = IN // (P * PACK)
+UNIT_TILES = 4
+UNITS_PER_EXAMPLE = S // (P * UNIT_TILES)
+N_UNITS = B * UNITS_PER_EXAMPLE
+J = P // NS
+GROUPS = R // J
+PREFETCH = 6
+TENSOR_EXAMPLES = 6
+VECTOR_EXAMPLES = (6, 7)
+SKILLS_PER_STEP = 4
+VECTOR_MIX_STEPS = Q * NS // SKILLS_PER_STEP
+
+FLOPS = 2 * B * S * IN * R + 2 * B * IN * R * NS
+
+
+def tile_skilledlora_pa_t_kernel(tc, x, weights, lora_a, out):
+    nc = tc.nc
+    x_units = x.rearrange("b (p h j) k -> b h p (j k)", h=UNITS_PER_EXAMPLE, j=UNIT_TILES)
+    out_units = out.rearrange("b (p h j) r -> b h p (j r)", h=UNITS_PER_EXAMPLE, j=UNIT_TILES)
+    la_splits = lora_a.rearrange("q s (p e) r -> q p s (e r)", e=2)
+
+    with ExitStack() as pools:
+        consts = pools.enter_context(tc.tile_pool(name="consts", bufs=1))
+        la_pool = pools.enter_context(tc.tile_pool(name="la", bufs=1))
+        x_pool = pools.enter_context(tc.tile_pool(name="x", bufs=PREFETCH + 2))
+        grouped_pool = pools.enter_context(tc.tile_pool(name="grouped", bufs=3))
+        codes_pool = pools.enter_context(tc.tile_pool(name="codes", bufs=6))
+        out_pool = pools.enter_context(tc.tile_pool(name="outs", bufs=3))
+        psum_x = pools.enter_context(tc.psum_pool(name="psum_x", bufs=4))
+        psum_o = pools.enter_context(tc.psum_pool(name="psum_o", bufs=2))
+        psum_p = pools.enter_context(tc.psum_pool(name="psum_p", bufs=2))
+
+        w_rows = consts.tile([P, B * Q * NS], BF16)
+        nc.scalar.dma_start(out=w_rows[:], in_=weights.rearrange("b q s -> (b q s)").partition_broadcast(P))
+        la_sb = la_pool.tile([P, Q, NS, 2 * R], BF16)
+        x_tiles = {}
+
+        def load_unit(i):
+            b, h = divmod(i, UNITS_PER_EXAMPLE)
+            x_sb = x_pool.tile([P, UNIT_TILES * IN], BF16)
+            nc.sync.dma_start(out=x_sb[:], in_=x_units[b, h])
+            x_tiles[i] = x_sb
+
+        for i in range(PREFETCH):
+            if i < Q:
+                nc.sync.dma_start(out=la_sb[:, i], in_=la_splits[i])
+            load_unit(i)
+
+        ident_f32 = consts.tile([P, P], F32)
+        make_identity(nc, ident_f32[:])
+        ident_bf16 = consts.tile([P, P], BF16)
+        make_identity(nc, ident_bf16[:])
+
+        skill_of_row = consts.tile([P, NS], F32)
+        nc.vector.tensor_reduce(
+            out=skill_of_row[:], in_=ident_f32[:].rearrange("p (s j) -> p s j", j=J), axis=AX.X, op=ALU.add
+        )
+        lane_of_row = consts.tile([P, J], F32)
+        nc.vector.tensor_reduce(
+            out=lane_of_row[:], in_=ident_f32[:].rearrange("p (s j) -> p j s", j=J), axis=AX.X, op=ALU.add
+        )
+        picked = consts.tile([P, B * Q, NS], F32)
+        nc.vector.tensor_tensor(
+            out=picked[:],
+            in0=w_rows[:].rearrange("p (c s) -> p c s", s=NS),
+            in1=skill_of_row[:].unsqueeze(1).to_broadcast([P, B * Q, NS]),
+            op=ALU.mult,
+        )
+        w_of_row = consts.tile([P, B, Q], F32)
+        nc.vector.tensor_reduce(out=w_of_row[:].rearrange("p b q -> p (b q)"), in_=picked[:], axis=AX.X, op=ALU.add)
+        w_block = consts.tile([P, Q, TENSOR_EXAMPLES, J], BF16)
+        for q in range(Q):
+            nc.vector.tensor_tensor(
+                out=w_block[:, q],
+                in0=lane_of_row[:].unsqueeze(1).to_broadcast([P, TENSOR_EXAMPLES, J]),
+                in1=w_of_row[:, 0:TENSOR_EXAMPLES, q].unsqueeze(2).to_broadcast([P, TENSOR_EXAMPLES, J]),
+                op=ALU.mult,
+            )
+        w_f32 = consts.tile([P, B, Q, NS], F32)
+        nc.vector.tensor_copy(out=w_f32[:].rearrange("p b q s -> p (b q s)"), in_=w_rows[:])
+
+        la_grouped = la_pool.tile([P, Q, 2 * GROUPS, NS, J], BF16)
+        la_t = la_pool.tile([P, Q, 2 * GROUPS, P], BF16)
+
+        def flip_split(q):
+            nc.vector.tensor_copy(out=la_grouped[:, q], in_=la_sb[:, q].rearrange("p s (c j) -> p c s j", j=J))
+            for e in range(2):
+                flipped = psum_p.tile([P, GROUPS, P], BF16, tag="prologue")
+                for rg in range(GROUPS):
+                    nc.tensor.transpose(
+                        flipped[:, rg, :],
+                        la_grouped[:, q, e * GROUPS + rg].rearrange("p s j -> p (s j)"),
+                        ident_bf16[:],
+                    )
+                nc.scalar.copy(out=la_t[:, q, e * GROUPS : (e + 1) * GROUPS, :], in_=flipped[:])
+
+        a_grouped = consts.tile([P, B * PASSES * R * PACK], BF16, align_bytes=64)
+        a_grouped_view = a_grouped[:].rearrange("p (b g r t) -> p b g r t", b=B, g=PASSES, t=PACK)
+        a_codes = consts.tile([P, B * PASSES * R], U32, align_bytes=64)
+        a_scales = consts.tile([P, B * PASSES * R], U8, align_bytes=64)
+
+        def mix_pass_on_tensor(g):
+            for rg in range(GROUPS):
+                mixed = psum_p.tile([P, PACK, TENSOR_EXAMPLES * J], F32, tag="prologue")
+                for u in range(2):
+                    for e in range(2):
+                        q = 2 * g + u
+                        nc.tensor.matmul(
+                            out=mixed[:, 2 * u + e, :],
+                            lhsT=la_t[:, q, e * GROUPS + rg, :],
+                            rhs=w_block[:, q].rearrange("p b j -> p (b j)"),
+                            start=True,
+                            stop=True,
+                        )
+                nc.scalar.copy(
+                    out=a_grouped_view[:, 0:TENSOR_EXAMPLES, g, rg * J : (rg + 1) * J, :],
+                    in_=mixed[:].rearrange("p t (b j) -> p b j t", j=J),
+                )
+
+        mix_sums = {}
+        for b in VECTOR_EXAMPLES:
+            mix_sum = consts.tile([P, Q * 2 * R], F32, name="mix_sum%d" % b)
+            mix_sums[b] = mix_sum
+
+        def mix_on_vector(step):
+            q, part = divmod(step, NS // SKILLS_PER_STEP)
+            cols = slice(q * 2 * R, (q + 1) * 2 * R)
+            for s in range(part * SKILLS_PER_STEP, (part + 1) * SKILLS_PER_STEP):
+                for b in VECTOR_EXAMPLES:
+                    if s == 0:
+                        nc.vector.tensor_scalar_mul(
+                            out=mix_sums[b][:, cols], in0=la_sb[:, q, s], scalar1=w_f32[:, b, q, s : s + 1]
+                        )
+                    else:
+                        nc.vector.scalar_tensor_tensor(
+                            out=mix_sums[b][:, cols],
+                            in0=la_sb[:, q, s],
+                            scalar=w_f32[:, b, q, s : s + 1],
+                            in1=mix_sums[b][:, cols],
+                            op0=ALU.mult,
+                            op1=ALU.add,
+                        )
+
+        def round_vector_mix():
+            for b in VECTOR_EXAMPLES:
+                nc.vector.tensor_copy(
+                    out=a_grouped_view[:, b],
+                    in_=mix_sums[b][:].rearrange("p (g t r) -> p g r t", g=PASSES, t=PACK),
+                )
+
+        def quantise_a_pair(pair):
+            words = 2 * PASSES * R
+            nc.vector.quantize_mx(
+                out=a_codes[:, pair * words : (pair + 1) * words].bitcast(FP8X4),
+                scales=a_scales[:, pair * words : (pair + 1) * words],
+                in_=a_grouped[:, pair * words * PACK : (pair + 1) * words * PACK],
+            )
+
+        grouped_tiles = {}
+        code_tiles = {}
+
+        def transpose_unit(i):
+            x_words = x_tiles[i][:].bitcast(F32)
+            x_grouped = grouped_pool.tile([P, UNIT_TILES * IN], BF16, align_bytes=64)
+            grouped_words = x_grouped[:].bitcast(F32).rearrange(
+                "p (j g r u) -> p j g r u", j=UNIT_TILES, g=PASSES, u=2
+            )
+            for j in range(UNIT_TILES):
+                flipped_x = psum_x.tile([P, Q, P], F32)
+                for q in range(Q):
+                    first = (j * Q + q) * P
+                    nc.tensor.transpose(flipped_x[:, q, :], x_words[:, first : first + P], ident_f32[:])
+                source = flipped_x[:].rearrange("p (g u) r -> p g r u", u=2)
+                nc.scalar.copy(out=grouped_words[:, j], in_=source)
+            grouped_tiles[i] = x_grouped
+
+        def quantise_unit(i):
+            x_codes = codes_pool.tile([P, UNIT_TILES * PASSES * P], U32, align_bytes=64)
+            x_scales = codes_pool.tile([P, UNIT_TILES * PASSES * P], U8, align_bytes=64)
+            nc.vector.quantize_mx(out=x_codes[:].bitcast(FP8X4), scales=x_scales[:], in_=grouped_tiles[i][:])
+            code_tiles[i] = (x_codes, x_scales)
+
+        def multiply_unit(i):
+            b, h = divmod(i, UNITS_PER_EXAMPLE)
+            x_codes, x_scales = code_tiles[i]
+            acc = psum_o.tile([P, UNIT_TILES, R], F32)
+            for j in range(UNIT_TILES):
+                for g in range(PASSES):
+                    x_cols = slice((j * PASSES + g) * P, (j * PASSES + g + 1) * P)
+                    a_cols = slice((b * PASSES + g) * R, (b * PASSES + g + 1) * R)
+                    nc.tensor.matmul_mx(
+                        out=acc[:, j, :],
+                        lhsT=x_codes[:, x_cols].bitcast(FP8X4),
+                        lhsT_scale=x_scales[:, x_cols],
+                        rhs=a_codes[:, a_cols].bitcast(FP8X4),
+                        rhs_scale=a_scales[:, a_cols],
+                        start=(g == 0),
+                        stop=(g == PASSES - 1),
+                    )
+            result = out_pool.tile([P, UNIT_TILES * R], F32)
+            if i < VECTOR_MIX_STEPS:
+                nc.scalar.copy(out=result[:], in_=acc[:].rearrange("p j r -> p (j r)"))
+            else:
+                nc.vector.tensor_copy(out=result[:], in_=acc[:].rearrange("p j r -> p (j r)"))
+            nc.sync.dma_start(out=out_units[b, h], in_=result[:])
+
+        multiplied = 0
+        for step in range(N_UNITS + 2):
+            if step + PREFETCH < N_UNITS:
+                load_unit(step + PREFETCH)
+            if step < Q:
+                flip_split(step)
+            if step < N_UNITS:
+                transpose_unit(step)
+            if step < Q and step % 2 == 1:
+                mix_pass_on_tensor(step // 2)
+            if step < VECTOR_MIX_STEPS:
+                mix_on_vector(step)
+            if 1 <= step <= N_UNITS:
+                quantise_unit(step - 1)
+            if step == Q - 1:
+                for pair in range(TENSOR_EXAMPLES // 2):
+                    quantise_a_pair(pair)
+            if step == VECTOR_MIX_STEPS:
+                round_vector_mix()
+                quantise_a_pair(TENSOR_EXAMPLES // 2)
+            if step >= Q:
+                for i in range(multiplied, step - 1):
+                    multiply_unit(i)
+                multiplied = step - 1

@@ -45,6 +45,7 @@ def tile_skilledlora_pa_t_kernel(tc, x, weights, lora_a, out):
         psum_x = pools.enter_context(tc.psum_pool(name="psum_x", bufs=4))
         psum_o = pools.enter_context(tc.psum_pool(name="psum_o", bufs=2))
         psum_p = pools.enter_context(tc.psum_pool(name="psum_p", bufs=2))
+        pools.enter_context(tc.manual_schedule())
 
         w_rows = consts.tile([P, B * Q * NS], BF16)
         nc.scalar.dma_start(out=w_rows[:], in_=weights.rearrange("b q s -> (b q s)").partition_broadcast(P))

@@ -21,10 +21,14 @@ N_UNITS = B * UNITS_PER_EXAMPLE
 J = P // NS
 GROUPS = R // J
 PREFETCH = 6
+MULTIPLY_LAG = 2
 TENSOR_EXAMPLES = 6
 VECTOR_EXAMPLES = (6, 7)
-SKILLS_PER_STEP = 4
-VECTOR_MIX_STEPS = Q * NS // SKILLS_PER_STEP
+TERMS = len(VECTOR_EXAMPLES) * Q * NS
+TERMS_BESIDE_A_SPLIT = 7
+TERMS_BESIDE_A_UNIT = 3
+VECTOR_MIX_STEPS = (TERMS - Q * TERMS_BESIDE_A_SPLIT) // TERMS_BESIDE_A_UNIT
+assert Q * TERMS_BESIDE_A_SPLIT + VECTOR_MIX_STEPS * TERMS_BESIDE_A_UNIT == TERMS
 
 FLOPS = 2 * B * S * IN * R + 2 * B * IN * R * NS
 
@@ -40,16 +44,18 @@ def tile_skilledlora_pa_t_kernel(tc, x, weights, lora_a, out):
         la_pool = pools.enter_context(tc.tile_pool(name="la", bufs=1))
         x_pool = pools.enter_context(tc.tile_pool(name="x", bufs=PREFETCH + 2))
         grouped_pool = pools.enter_context(tc.tile_pool(name="grouped", bufs=3))
-        codes_pool = pools.enter_context(tc.tile_pool(name="codes", bufs=6))
+        codes_pool = pools.enter_context(tc.tile_pool(name="codes", bufs=4))
         out_pool = pools.enter_context(tc.tile_pool(name="outs", bufs=3))
-        psum_x = pools.enter_context(tc.psum_pool(name="psum_x", bufs=4))
-        psum_o = pools.enter_context(tc.psum_pool(name="psum_o", bufs=2))
-        psum_p = pools.enter_context(tc.psum_pool(name="psum_p", bufs=2))
+        psum_work = pools.enter_context(tc.psum_pool(name="psum_work", bufs=6))
+        psum_acc = pools.enter_context(tc.psum_pool(name="psum_acc", bufs=2))
         pools.enter_context(tc.manual_schedule())
 
-        w_rows = consts.tile([P, B * Q * NS], BF16)
-        nc.scalar.dma_start(out=w_rows[:], in_=weights.rearrange("b q s -> (b q s)").partition_broadcast(P))
+        w_padded = consts.tile([P, B * Q * NS], BF16)
+        nc.vector.memset(w_padded[:], 0.0)
+        nc.sync.dma_start(out=w_padded[0:1, :], in_=weights.rearrange("(o b) q s -> o (b q s)", o=1))
         la_sb = la_pool.tile([P, Q, NS, 2 * R], BF16)
+        for q in range(Q):
+            nc.sync.dma_start(out=la_sb[:, q], in_=la_splits[q])
         x_tiles = {}
 
         def load_unit(i):
@@ -59,14 +65,19 @@ def tile_skilledlora_pa_t_kernel(tc, x, weights, lora_a, out):
             x_tiles[i] = x_sb
 
         for i in range(PREFETCH):
-            if i < Q:
-                nc.sync.dma_start(out=la_sb[:, i], in_=la_splits[i])
             load_unit(i)
 
         ident_f32 = consts.tile([P, P], F32)
         make_identity(nc, ident_f32[:])
         ident_bf16 = consts.tile([P, P], BF16)
         make_identity(nc, ident_bf16[:])
+        ones = consts.tile([P, P], BF16)
+        nc.vector.memset(ones[:], 1.0)
+
+        w_spread = psum_work.tile([P, B * Q * NS], F32, tag="work")
+        nc.tensor.matmul(out=w_spread[:], lhsT=ones[:], rhs=w_padded[:], start=True, stop=True)
+        w_f32 = consts.tile([P, B, Q, NS], F32)
+        nc.vector.tensor_copy(out=w_f32[:].rearrange("p b q s -> p (b q s)"), in_=w_spread[:])
 
         skill_of_row = consts.tile([P, NS], F32)
         nc.vector.tensor_reduce(
@@ -79,7 +90,7 @@ def tile_skilledlora_pa_t_kernel(tc, x, weights, lora_a, out):
         picked = consts.tile([P, B * Q, NS], F32)
         nc.vector.tensor_tensor(
             out=picked[:],
-            in0=w_rows[:].rearrange("p (c s) -> p c s", s=NS),
+            in0=w_f32[:].rearrange("p b q s -> p (b q) s"),
             in1=skill_of_row[:].unsqueeze(1).to_broadcast([P, B * Q, NS]),
             op=ALU.mult,
         )
@@ -93,8 +104,6 @@ def tile_skilledlora_pa_t_kernel(tc, x, weights, lora_a, out):
                 in1=w_of_row[:, 0:TENSOR_EXAMPLES, q].unsqueeze(2).to_broadcast([P, TENSOR_EXAMPLES, J]),
                 op=ALU.mult,
             )
-        w_f32 = consts.tile([P, B, Q, NS], F32)
-        nc.vector.tensor_copy(out=w_f32[:].rearrange("p b q s -> p (b q s)"), in_=w_rows[:])
 
         la_grouped = la_pool.tile([P, Q, 2 * GROUPS, NS, J], BF16)
         la_t = la_pool.tile([P, Q, 2 * GROUPS, P], BF16)
@@ -102,7 +111,7 @@ def tile_skilledlora_pa_t_kernel(tc, x, weights, lora_a, out):
         def flip_split(q):
             nc.vector.tensor_copy(out=la_grouped[:, q], in_=la_sb[:, q].rearrange("p s (c j) -> p c s j", j=J))
             for e in range(2):
-                flipped = psum_p.tile([P, GROUPS, P], BF16, tag="prologue")
+                flipped = psum_work.tile([P, GROUPS, P], BF16, tag="work")
                 for rg in range(GROUPS):
                     nc.tensor.transpose(
                         flipped[:, rg, :],
@@ -118,7 +127,7 @@ def tile_skilledlora_pa_t_kernel(tc, x, weights, lora_a, out):
 
         def mix_pass_on_tensor(g):
             for rg in range(GROUPS):
-                mixed = psum_p.tile([P, PACK, TENSOR_EXAMPLES * J], F32, tag="prologue")
+                mixed = psum_work.tile([P, PACK, TENSOR_EXAMPLES * J], F32, tag="work")
                 for u in range(2):
                     for e in range(2):
                         q = 2 * g + u
@@ -138,25 +147,24 @@ def tile_skilledlora_pa_t_kernel(tc, x, weights, lora_a, out):
         for b in VECTOR_EXAMPLES:
             mix_sum = consts.tile([P, Q * 2 * R], F32, name="mix_sum%d" % b)
             mix_sums[b] = mix_sum
+        terms = [(b, q, s) for q in range(Q) for s in range(NS) for b in VECTOR_EXAMPLES]
 
-        def mix_on_vector(step):
-            q, part = divmod(step, NS // SKILLS_PER_STEP)
-            cols = slice(q * 2 * R, (q + 1) * 2 * R)
-            for s in range(part * SKILLS_PER_STEP, (part + 1) * SKILLS_PER_STEP):
-                for b in VECTOR_EXAMPLES:
-                    if s == 0:
-                        nc.vector.tensor_scalar_mul(
-                            out=mix_sums[b][:, cols], in0=la_sb[:, q, s], scalar1=w_f32[:, b, q, s : s + 1]
-                        )
-                    else:
-                        nc.vector.scalar_tensor_tensor(
-                            out=mix_sums[b][:, cols],
-                            in0=la_sb[:, q, s],
-                            scalar=w_f32[:, b, q, s : s + 1],
-                            in1=mix_sums[b][:, cols],
-                            op0=ALU.mult,
-                            op1=ALU.add,
-                        )
+        def mix_on_vector(first, count):
+            for b, q, s in terms[first : first + count]:
+                cols = slice(q * 2 * R, (q + 1) * 2 * R)
+                if s == 0:
+                    nc.vector.tensor_scalar_mul(
+                        out=mix_sums[b][:, cols], in0=la_sb[:, q, s], scalar1=w_f32[:, b, q, s : s + 1]
+                    )
+                else:
+                    nc.vector.scalar_tensor_tensor(
+                        out=mix_sums[b][:, cols],
+                        in0=la_sb[:, q, s],
+                        scalar=w_f32[:, b, q, s : s + 1],
+                        in1=mix_sums[b][:, cols],
+                        op0=ALU.mult,
+                        op1=ALU.add,
+                    )
 
         def round_vector_mix():
             for b in VECTOR_EXAMPLES:
@@ -173,6 +181,14 @@ def tile_skilledlora_pa_t_kernel(tc, x, weights, lora_a, out):
                 in_=a_grouped[:, pair * words * PACK : (pair + 1) * words * PACK],
             )
 
+        for q in range(Q):
+            flip_split(q)
+            mix_on_vector(q * TERMS_BESIDE_A_SPLIT, TERMS_BESIDE_A_SPLIT)
+            if q % 2 == 1:
+                mix_pass_on_tensor(q // 2)
+        for pair in range(TENSOR_EXAMPLES // 2):
+            quantise_a_pair(pair)
+
         grouped_tiles = {}
         code_tiles = {}
 
@@ -183,12 +199,11 @@ def tile_skilledlora_pa_t_kernel(tc, x, weights, lora_a, out):
                 "p (j g r u) -> p j g r u", j=UNIT_TILES, g=PASSES, u=2
             )
             for j in range(UNIT_TILES):
-                flipped_x = psum_x.tile([P, Q, P], F32)
+                flipped_x = psum_work.tile([P, Q, P], F32, tag="work")
                 for q in range(Q):
                     first = (j * Q + q) * P
                     nc.tensor.transpose(flipped_x[:, q, :], x_words[:, first : first + P], ident_f32[:])
-                source = flipped_x[:].rearrange("p (g u) r -> p g r u", u=2)
-                nc.scalar.copy(out=grouped_words[:, j], in_=source)
+                nc.scalar.copy(out=grouped_words[:, j], in_=flipped_x[:].rearrange("p (g u) r -> p g r u", u=2))
             grouped_tiles[i] = x_grouped
 
         def quantise_unit(i):
@@ -200,7 +215,7 @@ def tile_skilledlora_pa_t_kernel(tc, x, weights, lora_a, out):
         def multiply_unit(i):
             b, h = divmod(i, UNITS_PER_EXAMPLE)
             x_codes, x_scales = code_tiles[i]
-            acc = psum_o.tile([P, UNIT_TILES, R], F32)
+            acc = psum_acc.tile([P, UNIT_TILES, R], F32)
             for j in range(UNIT_TILES):
                 for g in range(PASSES):
                     x_cols = slice((j * PASSES + g) * P, (j * PASSES + g + 1) * P)
@@ -215,33 +230,20 @@ def tile_skilledlora_pa_t_kernel(tc, x, weights, lora_a, out):
                         stop=(g == PASSES - 1),
                     )
             result = out_pool.tile([P, UNIT_TILES * R], F32)
-            if i < VECTOR_MIX_STEPS:
-                nc.scalar.copy(out=result[:], in_=acc[:].rearrange("p j r -> p (j r)"))
-            else:
-                nc.vector.tensor_copy(out=result[:], in_=acc[:].rearrange("p j r -> p (j r)"))
+            nc.vector.tensor_copy(out=result[:], in_=acc[:].rearrange("p j r -> p (j r)"))
             nc.sync.dma_start(out=out_units[b, h], in_=result[:])
 
-        multiplied = 0
-        for step in range(N_UNITS + 2):
+        for step in range(N_UNITS + MULTIPLY_LAG):
             if step + PREFETCH < N_UNITS:
                 load_unit(step + PREFETCH)
-            if step < Q:
-                flip_split(step)
             if step < N_UNITS:
                 transpose_unit(step)
-            if step < Q and step % 2 == 1:
-                mix_pass_on_tensor(step // 2)
             if step < VECTOR_MIX_STEPS:
-                mix_on_vector(step)
+                mix_on_vector(Q * TERMS_BESIDE_A_SPLIT + step * TERMS_BESIDE_A_UNIT, TERMS_BESIDE_A_UNIT)
             if 1 <= step <= N_UNITS:
                 quantise_unit(step - 1)
-            if step == Q - 1:
-                for pair in range(TENSOR_EXAMPLES // 2):
-                    quantise_a_pair(pair)
             if step == VECTOR_MIX_STEPS:
                 round_vector_mix()
                 quantise_a_pair(TENSOR_EXAMPLES // 2)
-            if step >= Q:
-                for i in range(multiplied, step - 1):
-                    multiply_unit(i)
-                multiplied = step - 1
+            if step >= MULTIPLY_LAG:
+                multiply_unit(step - MULTIPLY_LAG)

@@ -22,13 +22,14 @@ J = P // NS
 GROUPS = R // J
 PREFETCH = 6
 MULTIPLY_LAG = 2
+ROUND_UNITS = 2
 TENSOR_EXAMPLES = 6
 VECTOR_EXAMPLES = (6, 7)
 TERMS = len(VECTOR_EXAMPLES) * Q * NS
-TERMS_BESIDE_A_SPLIT = 7
-TERMS_BESIDE_A_UNIT = 3
-VECTOR_MIX_STEPS = (TERMS - Q * TERMS_BESIDE_A_SPLIT) // TERMS_BESIDE_A_UNIT
-assert Q * TERMS_BESIDE_A_SPLIT + VECTOR_MIX_STEPS * TERMS_BESIDE_A_UNIT == TERMS
+TERMS_BESIDE_A_PASS = 10
+TERMS_BESIDE_A_UNIT = 4
+VECTOR_MIX_STEPS = (TERMS - PASSES * TERMS_BESIDE_A_PASS) // TERMS_BESIDE_A_UNIT
+assert PASSES * TERMS_BESIDE_A_PASS + VECTOR_MIX_STEPS * TERMS_BESIDE_A_UNIT == TERMS
 
 FLOPS = 2 * B * S * IN * R + 2 * B * IN * R * NS
 
@@ -54,8 +55,6 @@ def tile_skilledlora_pa_t_kernel(tc, x, weights, lora_a, out):
         nc.vector.memset(w_padded[:], 0.0)
         nc.sync.dma_start(out=w_padded[0:1, :], in_=weights.rearrange("(o b) q s -> o (b q s)", o=1))
         la_sb = la_pool.tile([P, Q, NS, 2 * R], BF16)
-        for q in range(Q):
-            nc.sync.dma_start(out=la_sb[:, q], in_=la_splits[q])
         x_tiles = {}
 
         def load_unit(i):
@@ -64,7 +63,11 @@ def tile_skilledlora_pa_t_kernel(tc, x, weights, lora_a, out):
             nc.sync.dma_start(out=x_sb[:], in_=x_units[b, h])
             x_tiles[i] = x_sb
 
-        for i in range(PREFETCH):
+        for g in range(PASSES):
+            nc.sync.dma_start(out=la_sb[:, 2 * g], in_=la_splits[2 * g])
+            nc.sync.dma_start(out=la_sb[:, 2 * g + 1], in_=la_splits[2 * g + 1])
+            load_unit(g)
+        for i in range(PASSES, PREFETCH):
             load_unit(i)
 
         ident_f32 = consts.tile([P, P], F32)
@@ -108,8 +111,10 @@ def tile_skilledlora_pa_t_kernel(tc, x, weights, lora_a, out):
         la_grouped = la_pool.tile([P, Q, 2 * GROUPS, NS, J], BF16)
         la_t = la_pool.tile([P, Q, 2 * GROUPS, P], BF16)
 
-        def flip_split(q):
+        def regroup_split(q):
             nc.vector.tensor_copy(out=la_grouped[:, q], in_=la_sb[:, q].rearrange("p s (c j) -> p c s j", j=J))
+
+        def flip_split(q):
             for e in range(2):
                 flipped = psum_work.tile([P, GROUPS, P], BF16, tag="work")
                 for rg in range(GROUPS):
@@ -118,7 +123,7 @@ def tile_skilledlora_pa_t_kernel(tc, x, weights, lora_a, out):
                         la_grouped[:, q, e * GROUPS + rg].rearrange("p s j -> p (s j)"),
                         ident_bf16[:],
                     )
-                nc.scalar.copy(out=la_t[:, q, e * GROUPS : (e + 1) * GROUPS, :], in_=flipped[:])
+                nc.vector.tensor_copy(out=la_t[:, q, e * GROUPS : (e + 1) * GROUPS, :], in_=flipped[:])
 
         a_grouped = consts.tile([P, B * PASSES * R * PACK], BF16, align_bytes=64)
         a_grouped_view = a_grouped[:].rearrange("p (b g r t) -> p b g r t", b=B, g=PASSES, t=PACK)
@@ -181,14 +186,6 @@ def tile_skilledlora_pa_t_kernel(tc, x, weights, lora_a, out):
                 in_=a_grouped[:, pair * words * PACK : (pair + 1) * words * PACK],
             )
 
-        for q in range(Q):
-            flip_split(q)
-            mix_on_vector(q * TERMS_BESIDE_A_SPLIT, TERMS_BESIDE_A_SPLIT)
-            if q % 2 == 1:
-                mix_pass_on_tensor(q // 2)
-        for pair in range(TENSOR_EXAMPLES // 2):
-            quantise_a_pair(pair)
-
         grouped_tiles = {}
         code_tiles = {}
 
@@ -230,20 +227,38 @@ def tile_skilledlora_pa_t_kernel(tc, x, weights, lora_a, out):
                         stop=(g == PASSES - 1),
                     )
             result = out_pool.tile([P, UNIT_TILES * R], F32)
-            nc.vector.tensor_copy(out=result[:], in_=acc[:].rearrange("p j r -> p (j r)"))
+            nc.scalar.copy(out=result[:], in_=acc[:].rearrange("p j r -> p (j r)"))
             nc.sync.dma_start(out=out_units[b, h], in_=result[:])
 
-        for step in range(N_UNITS + MULTIPLY_LAG):
-            if step + PREFETCH < N_UNITS:
-                load_unit(step + PREFETCH)
-            if step < N_UNITS:
-                transpose_unit(step)
-            if step < VECTOR_MIX_STEPS:
-                mix_on_vector(Q * TERMS_BESIDE_A_SPLIT + step * TERMS_BESIDE_A_UNIT, TERMS_BESIDE_A_UNIT)
-            if 1 <= step <= N_UNITS:
-                quantise_unit(step - 1)
-            if step == VECTOR_MIX_STEPS:
-                round_vector_mix()
-                quantise_a_pair(TENSOR_EXAMPLES // 2)
-            if step >= MULTIPLY_LAG:
+        for g in range(PASSES):
+            regroup_split(2 * g)
+            regroup_split(2 * g + 1)
+            flip_split(2 * g)
+            flip_split(2 * g + 1)
+            transpose_unit(g)
+            mix_pass_on_tensor(g)
+            mix_on_vector(g * TERMS_BESIDE_A_PASS, TERMS_BESIDE_A_PASS)
+            if g >= 1:
+                quantise_unit(g - 1)
+        for pair in range(TENSOR_EXAMPLES // 2):
+            quantise_a_pair(pair)
+
+        for first_step in range(PASSES, N_UNITS + MULTIPLY_LAG, ROUND_UNITS):
+            steps = range(first_step, first_step + ROUND_UNITS)
+            for step in steps:
+                if step + PREFETCH - PASSES < N_UNITS:
+                    load_unit(step + PREFETCH - PASSES)
+                if step < N_UNITS:
+                    transpose_unit(step)
+            for step in steps:
+                if step - PASSES < VECTOR_MIX_STEPS:
+                    mix_on_vector(
+                        PASSES * TERMS_BESIDE_A_PASS + (step - PASSES) * TERMS_BESIDE_A_UNIT, TERMS_BESIDE_A_UNIT
+                    )
+                if step <= N_UNITS:
+                    quantise_unit(step - 1)
+                if step - PASSES == VECTOR_MIX_STEPS:
+                    round_vector_mix()
+                    quantise_a_pair(TENSOR_EXAMPLES // 2)
+            for step in steps:
                 multiply_unit(step - MULTIPLY_LAG)

@@ -52,8 +52,7 @@ def tile_skilledlora_pa_t_kernel(tc, x, weights, lora_a, out):
         pools.enter_context(tc.manual_schedule())
 
         w_padded = consts.tile([P, B * Q * NS], BF16)
-        nc.vector.memset(w_padded[:], 0.0)
-        nc.sync.dma_start(out=w_padded[0:1, :], in_=weights.rearrange("(o b) q s -> o (b q s)", o=1))
+        nc.gpsimd.memset(w_padded[:], 0.0)
         la_sb = la_pool.tile([P, Q, NS, 2 * R], BF16)
         x_tiles = {}
 
@@ -65,6 +64,8 @@ def tile_skilledlora_pa_t_kernel(tc, x, weights, lora_a, out):
 
         for g in range(PASSES):
             nc.sync.dma_start(out=la_sb[:, 2 * g], in_=la_splits[2 * g])
+            if g == 0:
+                nc.sync.dma_start(out=w_padded[0:1, :], in_=weights.rearrange("(o b) q s -> o (b q s)", o=1))
             nc.sync.dma_start(out=la_sb[:, 2 * g + 1], in_=la_splits[2 * g + 1])
             load_unit(g)
         for i in range(PASSES, PREFETCH):
@@ -77,11 +78,6 @@ def tile_skilledlora_pa_t_kernel(tc, x, weights, lora_a, out):
         ones = consts.tile([P, P], BF16)
         nc.vector.memset(ones[:], 1.0)
 
-        w_spread = psum_work.tile([P, B * Q * NS], F32, tag="work")
-        nc.tensor.matmul(out=w_spread[:], lhsT=ones[:], rhs=w_padded[:], start=True, stop=True)
-        w_f32 = consts.tile([P, B, Q, NS], F32)
-        nc.vector.tensor_copy(out=w_f32[:].rearrange("p b q s -> p (b q s)"), in_=w_spread[:])
-
         skill_of_row = consts.tile([P, NS], F32)
         nc.vector.tensor_reduce(
             out=skill_of_row[:], in_=ident_f32[:].rearrange("p (s j) -> p s j", j=J), axis=AX.X, op=ALU.add
@@ -90,6 +86,19 @@ def tile_skilledlora_pa_t_kernel(tc, x, weights, lora_a, out):
         nc.vector.tensor_reduce(
             out=lane_of_row[:], in_=ident_f32[:].rearrange("p (s j) -> p j s", j=J), axis=AX.X, op=ALU.add
         )
+        la_grouped = la_pool.tile([P, Q, 2 * GROUPS, NS, J], BF16)
+
+        def regroup_split(q):
+            nc.vector.tensor_copy(out=la_grouped[:, q], in_=la_sb[:, q].rearrange("p s (c j) -> p c s j", j=J))
+
+        regroup_split(0)
+        regroup_split(1)
+
+        w_spread = psum_work.tile([P, B * Q * NS], F32, tag="work")
+        nc.tensor.matmul(out=w_spread[:], lhsT=ones[:], rhs=w_padded[:], start=True, stop=True)
+        w_f32 = consts.tile([P, B, Q, NS], F32)
+        nc.vector.tensor_copy(out=w_f32[:].rearrange("p b q s -> p (b q s)"), in_=w_spread[:])
+
         picked = consts.tile([P, B * Q, NS], F32)
         nc.vector.tensor_tensor(
             out=picked[:],
@@ -108,11 +117,7 @@ def tile_skilledlora_pa_t_kernel(tc, x, weights, lora_a, out):
                 op=ALU.mult,
             )
 
-        la_grouped = la_pool.tile([P, Q, 2 * GROUPS, NS, J], BF16)
         la_t = la_pool.tile([P, Q, 2 * GROUPS, P], BF16)
-
-        def regroup_split(q):
-            nc.vector.tensor_copy(out=la_grouped[:, q], in_=la_sb[:, q].rearrange("p s (c j) -> p c s j", j=J))
 
         def flip_split(q):
             for e in range(2):
@@ -206,7 +211,13 @@ def tile_skilledlora_pa_t_kernel(tc, x, weights, lora_a, out):
         def quantise_unit(i):
             x_codes = codes_pool.tile([P, UNIT_TILES * PASSES * P], U32, align_bytes=64)
             x_scales = codes_pool.tile([P, UNIT_TILES * PASSES * P], U8, align_bytes=64)
-            nc.vector.quantize_mx(out=x_codes[:].bitcast(FP8X4), scales=x_scales[:], in_=grouped_tiles[i][:])
+            words = UNIT_TILES * PASSES * P // 2
+            for c in range(2):
+                nc.vector.quantize_mx(
+                    out=x_codes[:, c * words : (c + 1) * words].bitcast(FP8X4),
+                    scales=x_scales[:, c * words : (c + 1) * words],
+                    in_=grouped_tiles[i][:, c * words * PACK : (c + 1) * words * PACK],
+                )
             code_tiles[i] = (x_codes, x_scales)
 
         def multiply_unit(i):
@@ -227,15 +238,19 @@ def tile_skilledlora_pa_t_kernel(tc, x, weights, lora_a, out):
                         stop=(g == PASSES - 1),
                     )
             result = out_pool.tile([P, UNIT_TILES * R], F32)
-            nc.scalar.copy(out=result[:], in_=acc[:].rearrange("p j r -> p (j r)"))
+            if i % 2 == 0:
+                nc.scalar.copy(out=result[:], in_=acc[:].rearrange("p j r -> p (j r)"))
+            else:
+                nc.vector.tensor_copy(out=result[:], in_=acc[:].rearrange("p j r -> p (j r)"))
             nc.sync.dma_start(out=out_units[b, h], in_=result[:])
 
         for g in range(PASSES):
-            regroup_split(2 * g)
-            regroup_split(2 * g + 1)
             flip_split(2 * g)
             flip_split(2 * g + 1)
             transpose_unit(g)
+            if g + 1 < PASSES:
+                regroup_split(2 * g + 2)
+                regroup_split(2 * g + 3)
             mix_pass_on_tensor(g)
             mix_on_vector(g * TERMS_BESIDE_A_PASS, TERMS_BESIDE_A_PASS)
             if g >= 1:

@@ -19,17 +19,12 @@ UNIT_TILES = 4
 UNITS_PER_EXAMPLE = S // (P * UNIT_TILES)
 N_UNITS = B * UNITS_PER_EXAMPLE
 J = P // NS
-GROUPS = R // J
-PREFETCH = 6
-MULTIPLY_LAG = 2
-ROUND_UNITS = 2
+LANE_RANKS = J // 2
+C = 16
+C_BANK = 4
 TENSOR_EXAMPLES = 6
 VECTOR_EXAMPLES = (6, 7)
-TERMS = len(VECTOR_EXAMPLES) * Q * NS
-TERMS_BESIDE_A_PASS = 10
-TERMS_BESIDE_A_UNIT = 4
-VECTOR_MIX_STEPS = (TERMS - PASSES * TERMS_BESIDE_A_PASS) // TERMS_BESIDE_A_UNIT
-assert PASSES * TERMS_BESIDE_A_PASS + VECTOR_MIX_STEPS * TERMS_BESIDE_A_UNIT == TERMS
+X_BUFS = 10
 
 FLOPS = 2 * B * S * IN * R + 2 * B * IN * R * NS
 
@@ -42,18 +37,22 @@ def tile_skilledlora_pa_t_kernel(tc, x, weights, lora_a, out):
 
     with ExitStack() as pools:
         consts = pools.enter_context(tc.tile_pool(name="consts", bufs=1))
-        la_pool = pools.enter_context(tc.tile_pool(name="la", bufs=1))
-        x_pool = pools.enter_context(tc.tile_pool(name="x", bufs=PREFETCH + 2))
-        grouped_pool = pools.enter_context(tc.tile_pool(name="grouped", bufs=3))
-        codes_pool = pools.enter_context(tc.tile_pool(name="codes", bufs=4))
-        out_pool = pools.enter_context(tc.tile_pool(name="outs", bufs=3))
+        x_pool = pools.enter_context(tc.tile_pool(name="x", bufs=X_BUFS))
+        grouped_pool = pools.enter_context(tc.tile_pool(name="grouped", bufs=4))
+        codes_pool = pools.enter_context(tc.tile_pool(name="codes", bufs=6))
+        out_pool = pools.enter_context(tc.tile_pool(name="outs", bufs=6))
         psum_work = pools.enter_context(tc.psum_pool(name="psum_work", bufs=6))
         psum_acc = pools.enter_context(tc.psum_pool(name="psum_acc", bufs=2))
         pools.enter_context(tc.manual_schedule())
 
-        w_padded = consts.tile([P, B * Q * NS], BF16)
-        nc.gpsimd.memset(w_padded[:], 0.0)
-        la_sb = la_pool.tile([P, Q, NS, 2 * R], BF16)
+        scalar_copy = nc.scalar.copy
+        vector_copy = nc.vector.tensor_copy
+
+        w_rows = consts.tile([P, NS], BF16)
+        nc.gpsimd.memset(w_rows[:], 0.0)
+        w_line = consts.tile([P, len(VECTOR_EXAMPLES) * Q * NS], BF16)
+        nc.gpsimd.memset(w_line[:], 0.0)
+        la_sb = consts.tile([P, Q, NS * 2 * R], BF16)
         x_tiles = {}
 
         def load_unit(i):
@@ -62,13 +61,20 @@ def tile_skilledlora_pa_t_kernel(tc, x, weights, lora_a, out):
             nc.sync.dma_start(out=x_sb[:], in_=x_units[b, h])
             x_tiles[i] = x_sb
 
-        for g in range(PASSES):
-            nc.sync.dma_start(out=la_sb[:, 2 * g], in_=la_splits[2 * g])
-            if g == 0:
-                nc.sync.dma_start(out=w_padded[0:1, :], in_=weights.rearrange("(o b) q s -> o (b q s)", o=1))
-            nc.sync.dma_start(out=la_sb[:, 2 * g + 1], in_=la_splits[2 * g + 1])
-            load_unit(g)
-        for i in range(PASSES, PREFETCH):
+        def load_split(q):
+            nc.sync.dma_start(out=la_sb[:, q].rearrange("p (s c) -> p s c", s=NS), in_=la_splits[q])
+
+        nc.sync.dma_start(out=w_rows[0 : B * Q, :], in_=weights.rearrange("b q s -> (b q) s"))
+        nc.sync.dma_start(
+            out=w_line[0:1, :],
+            in_=weights[VECTOR_EXAMPLES[0] : B].rearrange("(o b) q s -> o (b q s)", o=1),
+        )
+        load_split(0)
+        load_split(1)
+        load_unit(0)
+        load_split(2)
+        load_split(3)
+        for i in range(1, X_BUFS):
             load_unit(i)
 
         ident_f32 = consts.tile([P, P], F32)
@@ -77,103 +83,105 @@ def tile_skilledlora_pa_t_kernel(tc, x, weights, lora_a, out):
         make_identity(nc, ident_bf16[:])
         ones = consts.tile([P, P], BF16)
         nc.vector.memset(ones[:], 1.0)
-
-        skill_of_row = consts.tile([P, NS], F32)
-        nc.vector.tensor_reduce(
-            out=skill_of_row[:], in_=ident_f32[:].rearrange("p (s j) -> p s j", j=J), axis=AX.X, op=ALU.add
-        )
         lane_of_row = consts.tile([P, J], F32)
         nc.vector.tensor_reduce(
-            out=lane_of_row[:], in_=ident_f32[:].rearrange("p (s j) -> p j s", j=J), axis=AX.X, op=ALU.add
+            out=lane_of_row[:].rearrange("p (r e) -> p r e", e=2),
+            in_=ident_f32[:].rearrange("p (s e r) -> p r e s", s=NS, e=2),
+            axis=AX.X,
+            op=ALU.add,
         )
-        la_grouped = la_pool.tile([P, Q, 2 * GROUPS, NS, J], BF16)
 
-        def regroup_split(q):
-            nc.vector.tensor_copy(out=la_grouped[:, q], in_=la_sb[:, q].rearrange("p s (c j) -> p c s j", j=J))
+        la_t = consts.tile([P, Q, C, P], BF16)
 
-        regroup_split(0)
-        regroup_split(1)
+        def flip_split(q, engines):
+            la_lanes = la_sb[:, q].rearrange("p (m c) -> p m c", c=C)
+            for half in range(2):
+                flipped = psum_work.tile([P, C // 2, P], BF16, tag="work")
+                for k in range(C // 2):
+                    nc.tensor.transpose(flipped[:, k, :], la_lanes[:, :, half * C // 2 + k], ident_bf16[:])
+                engines[half](out=la_t[:, q, half * C // 2 : (half + 1) * C // 2, :], in_=flipped[:])
 
-        w_spread = psum_work.tile([P, B * Q * NS], F32, tag="work")
-        nc.tensor.matmul(out=w_spread[:], lhsT=ones[:], rhs=w_padded[:], start=True, stop=True)
-        w_f32 = consts.tile([P, B, Q, NS], F32)
-        nc.vector.tensor_copy(out=w_f32[:].rearrange("p b q s -> p (b q s)"), in_=w_spread[:])
+        def tensor_examples(q):
+            return TENSOR_EXAMPLES + 1 if q == 0 else TENSOR_EXAMPLES
 
-        picked = consts.tile([P, B * Q, NS], F32)
-        nc.vector.tensor_tensor(
-            out=picked[:],
-            in0=w_f32[:].rearrange("p b q s -> p (b q) s"),
-            in1=skill_of_row[:].unsqueeze(1).to_broadcast([P, B * Q, NS]),
-            op=ALU.mult,
-        )
-        w_of_row = consts.tile([P, B, Q], F32)
-        nc.vector.tensor_reduce(out=w_of_row[:].rearrange("p b q -> p (b q)"), in_=picked[:], axis=AX.X, op=ALU.add)
-        w_block = consts.tile([P, Q, TENSOR_EXAMPLES, J], BF16)
-        for q in range(Q):
-            nc.vector.tensor_tensor(
-                out=w_block[:, q],
-                in0=lane_of_row[:].unsqueeze(1).to_broadcast([P, TENSOR_EXAMPLES, J]),
-                in1=w_of_row[:, 0:TENSOR_EXAMPLES, q].unsqueeze(2).to_broadcast([P, TENSOR_EXAMPLES, J]),
-                op=ALU.mult,
-            )
+        w_rep = consts.tile([P, NS, J], BF16)
+        w_row = consts.tile([P, B * Q], F32)
+        w_block = consts.tile([P, Q, TENSOR_EXAMPLES + 1, J], BF16)
+        w_f32 = consts.tile([P, len(VECTOR_EXAMPLES), Q, NS], F32)
 
-        la_t = la_pool.tile([P, Q, 2 * GROUPS, P], BF16)
+        def turn_weights():
+            nc.vector.tensor_copy(out=w_rep[:], in_=w_rows[:].unsqueeze(2).to_broadcast([P, NS, J]))
 
-        def flip_split(q):
-            for e in range(2):
-                flipped = psum_work.tile([P, GROUPS, P], BF16, tag="work")
-                for rg in range(GROUPS):
-                    nc.tensor.transpose(
-                        flipped[:, rg, :],
-                        la_grouped[:, q, e * GROUPS + rg].rearrange("p s j -> p (s j)"),
-                        ident_bf16[:],
-                    )
-                nc.vector.tensor_copy(out=la_t[:, q, e * GROUPS : (e + 1) * GROUPS, :], in_=flipped[:])
+        def spread_weights():
+            w_turned = psum_work.tile([P, P], BF16, tag="work")
+            nc.tensor.transpose(w_turned[:], w_rep[:].rearrange("p s j -> p (s j)"), ident_bf16[:])
+            w_spread = psum_work.tile([P, len(VECTOR_EXAMPLES) * Q * NS], F32, tag="work")
+            nc.tensor.matmul(out=w_spread[:], lhsT=ones[:], rhs=w_line[:], start=True, stop=True)
+            nc.vector.tensor_copy(out=w_row[:], in_=w_turned[:, 0 : B * Q])
+            nc.vector.tensor_copy(out=w_f32[:].rearrange("p b q s -> p (b q s)"), in_=w_spread[:])
+            w_row_view = w_row[:].rearrange("p (b q) -> p b q", q=Q)
+            for q in range(Q):
+                n = tensor_examples(q)
+                nc.vector.tensor_tensor(
+                    out=w_block[:, q, 0:n],
+                    in0=lane_of_row[:].unsqueeze(1).to_broadcast([P, n, J]),
+                    in1=w_row_view[:, 0:n, q].unsqueeze(2).to_broadcast([P, n, J]),
+                    op=ALU.mult,
+                )
 
-        a_grouped = consts.tile([P, B * PASSES * R * PACK], BF16, align_bytes=64)
-        a_grouped_view = a_grouped[:].rearrange("p (b g r t) -> p b g r t", b=B, g=PASSES, t=PACK)
-        a_codes = consts.tile([P, B * PASSES * R], U32, align_bytes=64)
-        a_scales = consts.tile([P, B * PASSES * R], U8, align_bytes=64)
+        a_grouped = consts.tile([P, PASSES * B * R * PACK], BF16, align_bytes=64)
+        a_grouped_runs = a_grouped[:].rearrange("p (g k c) -> p g k c", g=PASSES, c=C * PACK)
+        a_grouped_view = a_grouped[:].rearrange("p (g b r t) -> p b g r t", g=PASSES, b=B, t=PACK)
+        a_codes = consts.tile([P, PASSES * B * R], U32, align_bytes=64)
+        a_scales = consts.tile([P, PASSES * B * R], U8, align_bytes=64)
+        KT = TENSOR_EXAMPLES * LANE_RANKS
 
-        def mix_pass_on_tensor(g):
-            for rg in range(GROUPS):
-                mixed = psum_work.tile([P, PACK, TENSOR_EXAMPLES * J], F32, tag="work")
+        def mix_bank(g, bank, copy):
+            mixed = psum_work.tile([P, (TENSOR_EXAMPLES + 1) * LANE_RANKS * C_BANK * PACK], BF16, tag="work")
+            mixed_view = mixed[:].rearrange("p (k c u e) -> p k c u e", c=C_BANK, u=2, e=2)
+            for c in range(C_BANK):
                 for u in range(2):
-                    for e in range(2):
-                        q = 2 * g + u
-                        nc.tensor.matmul(
-                            out=mixed[:, 2 * u + e, :],
-                            lhsT=la_t[:, q, e * GROUPS + rg, :],
-                            rhs=w_block[:, q].rearrange("p b j -> p (b j)"),
-                            start=True,
-                            stop=True,
-                        )
+                    q = 2 * g + u
+                    n = tensor_examples(q)
+                    nc.tensor.matmul(
+                        out=mixed_view[:, 0 : n * LANE_RANKS, c, u, :],
+                        lhsT=la_t[:, q, bank * C_BANK + c, :],
+                        rhs=w_block[:, q, 0:n].rearrange("p b (r e) -> p (b r) e", e=2),
+                        start=True,
+                        stop=True,
+                    )
+            run = C_BANK * PACK
+            copy(
+                out=a_grouped_runs[:, g, 0:KT, bank * run : (bank + 1) * run],
+                in_=mixed[:].rearrange("p (k c) -> p k c", c=run)[:, 0:KT],
+            )
+            if g == 0:
                 nc.scalar.copy(
-                    out=a_grouped_view[:, 0:TENSOR_EXAMPLES, g, rg * J : (rg + 1) * J, :],
-                    in_=mixed[:].rearrange("p t (b j) -> p b j t", j=J),
+                    out=mix_sums[TENSOR_EXAMPLES][:, 0 : 2 * R].rearrange("p (e r c) -> p e r c", e=2, c=C)[
+                        :, :, :, bank * C_BANK : (bank + 1) * C_BANK
+                    ],
+                    in_=mixed_view[:, KT : KT + LANE_RANKS, :, 0, :].rearrange("p r c e -> p e r c"),
                 )
 
         mix_sums = {}
         for b in VECTOR_EXAMPLES:
             mix_sum = consts.tile([P, Q * 2 * R], F32, name="mix_sum%d" % b)
             mix_sums[b] = mix_sum
-        terms = [(b, q, s) for q in range(Q) for s in range(NS) for b in VECTOR_EXAMPLES]
+        terms = [(b, q, s) for s in range(NS) for b, q in ((7, 0), (6, 1), (7, 1))]
+        terms += [(b, q, s) for q in (2, 3) for s in range(NS) for b in VECTOR_EXAMPLES]
 
-        def mix_on_vector(first, count):
-            for b, q, s in terms[first : first + count]:
+        def mix_on_vector(count):
+            for k in range(min(count, len(terms))):
+                b, q, s = terms.pop(0)
                 cols = slice(q * 2 * R, (q + 1) * 2 * R)
+                la = la_sb[:, q, s * 2 * R : (s + 1) * 2 * R]
+                w = w_f32[:, b - VECTOR_EXAMPLES[0], q, s : s + 1]
                 if s == 0:
-                    nc.vector.tensor_scalar_mul(
-                        out=mix_sums[b][:, cols], in0=la_sb[:, q, s], scalar1=w_f32[:, b, q, s : s + 1]
-                    )
+                    nc.vector.tensor_scalar_mul(out=mix_sums[b][:, cols], in0=la, scalar1=w)
                 else:
                     nc.vector.scalar_tensor_tensor(
-                        out=mix_sums[b][:, cols],
-                        in0=la_sb[:, q, s],
-                        scalar=w_f32[:, b, q, s : s + 1],
-                        in1=mix_sums[b][:, cols],
-                        op0=ALU.mult,
-                        op1=ALU.add,
+                        out=mix_sums[b][:, cols], in0=la, scalar=w, in1=mix_sums[b][:, cols],
+                        op0=ALU.mult, op1=ALU.add,
                     )
 
         def round_vector_mix():
@@ -183,51 +191,52 @@ def tile_skilledlora_pa_t_kernel(tc, x, weights, lora_a, out):
                     in_=mix_sums[b][:].rearrange("p (g t r) -> p g r t", g=PASSES, t=PACK),
                 )
 
-        def quantise_a_pair(pair):
-            words = 2 * PASSES * R
-            nc.vector.quantize_mx(
-                out=a_codes[:, pair * words : (pair + 1) * words].bitcast(FP8X4),
-                scales=a_scales[:, pair * words : (pair + 1) * words],
-                in_=a_grouped[:, pair * words * PACK : (pair + 1) * words * PACK],
-            )
+        def quantise_a(g, first, count):
+            cols = slice((g * B + first) * R, (g * B + first + count) * R)
+            wide = slice((g * B + first) * R * PACK, (g * B + first + count) * R * PACK)
+            nc.vector.quantize_mx(out=a_codes[:, cols].bitcast(FP8X4), scales=a_scales[:, cols], in_=a_grouped[:, wide])
 
         grouped_tiles = {}
         code_tiles = {}
 
-        def transpose_unit(i):
+        def transpose_tile(i, j, copy):
+            if j == 0:
+                x_grouped = grouped_pool.tile([P, UNIT_TILES * IN], BF16, align_bytes=64)
+                grouped_tiles[i] = x_grouped
             x_words = x_tiles[i][:].bitcast(F32)
-            x_grouped = grouped_pool.tile([P, UNIT_TILES * IN], BF16, align_bytes=64)
-            grouped_words = x_grouped[:].bitcast(F32).rearrange(
+            grouped_words = grouped_tiles[i][:].bitcast(F32).rearrange(
                 "p (j g r u) -> p j g r u", j=UNIT_TILES, g=PASSES, u=2
             )
-            for j in range(UNIT_TILES):
-                flipped_x = psum_work.tile([P, Q, P], F32, tag="work")
-                for q in range(Q):
-                    first = (j * Q + q) * P
-                    nc.tensor.transpose(flipped_x[:, q, :], x_words[:, first : first + P], ident_f32[:])
-                nc.scalar.copy(out=grouped_words[:, j], in_=flipped_x[:].rearrange("p (g u) r -> p g r u", u=2))
-            grouped_tiles[i] = x_grouped
+            flipped_x = psum_work.tile([P, Q, P], F32, tag="work")
+            for q in range(Q):
+                first = (j * Q + q) * P
+                nc.tensor.transpose(flipped_x[:, q, :], x_words[:, first : first + P], ident_f32[:])
+            copy(out=grouped_words[:, j], in_=flipped_x[:].rearrange("p (g u) r -> p g r u", u=2))
 
-        def quantise_unit(i):
+        def transpose_unit(i, vector_tiles=()):
+            for j in range(UNIT_TILES):
+                transpose_tile(i, j, vector_copy if j in vector_tiles else scalar_copy)
+
+        def quantise_unit(i, parts=1):
             x_codes = codes_pool.tile([P, UNIT_TILES * PASSES * P], U32, align_bytes=64)
             x_scales = codes_pool.tile([P, UNIT_TILES * PASSES * P], U8, align_bytes=64)
-            words = UNIT_TILES * PASSES * P // 2
-            for c in range(2):
+            code_tiles[i] = (x_codes, x_scales)
+            words = UNIT_TILES * PASSES * P // parts
+            for c in range(parts):
                 nc.vector.quantize_mx(
                     out=x_codes[:, c * words : (c + 1) * words].bitcast(FP8X4),
                     scales=x_scales[:, c * words : (c + 1) * words],
                     in_=grouped_tiles[i][:, c * words * PACK : (c + 1) * words * PACK],
                 )
-            code_tiles[i] = (x_codes, x_scales)
 
-        def multiply_unit(i):
+        def multiply_unit(i, copy):
             b, h = divmod(i, UNITS_PER_EXAMPLE)
             x_codes, x_scales = code_tiles[i]
             acc = psum_acc.tile([P, UNIT_TILES, R], F32)
             for j in range(UNIT_TILES):
                 for g in range(PASSES):
                     x_cols = slice((j * PASSES + g) * P, (j * PASSES + g + 1) * P)
-                    a_cols = slice((b * PASSES + g) * R, (b * PASSES + g + 1) * R)
+                    a_cols = slice((g * B + b) * R, (g * B + b + 1) * R)
                     nc.tensor.matmul_mx(
                         out=acc[:, j, :],
                         lhsT=x_codes[:, x_cols].bitcast(FP8X4),
@@ -238,42 +247,57 @@ def tile_skilledlora_pa_t_kernel(tc, x, weights, lora_a, out):
                         stop=(g == PASSES - 1),
                     )
             result = out_pool.tile([P, UNIT_TILES * R], F32)
-            if i % 2 == 0:
-                nc.scalar.copy(out=result[:], in_=acc[:].rearrange("p j r -> p (j r)"))
-            else:
-                nc.vector.tensor_copy(out=result[:], in_=acc[:].rearrange("p j r -> p (j r)"))
+            copy(out=result[:], in_=acc[:].rearrange("p j r -> p (j r)"))
             nc.sync.dma_start(out=out_units[b, h], in_=result[:])
 
-        for g in range(PASSES):
-            flip_split(2 * g)
-            flip_split(2 * g + 1)
-            transpose_unit(g)
-            if g + 1 < PASSES:
-                regroup_split(2 * g + 2)
-                regroup_split(2 * g + 3)
-            mix_pass_on_tensor(g)
-            mix_on_vector(g * TERMS_BESIDE_A_PASS, TERMS_BESIDE_A_PASS)
-            if g >= 1:
-                quantise_unit(g - 1)
-        for pair in range(TENSOR_EXAMPLES // 2):
-            quantise_a_pair(pair)
+        turn_weights()
+        flip_split(0, (scalar_copy, vector_copy))
+        spread_weights()
+        flip_split(1, (scalar_copy, vector_copy))
+        mix_on_vector(5)
+        transpose_unit(0)
+        mix_bank(0, 0, vector_copy)
+        mix_bank(0, 1, vector_copy)
+        flip_split(2, (scalar_copy, vector_copy))
+        mix_bank(0, 2, vector_copy)
+        mix_bank(0, 3, vector_copy)
+        quantise_unit(0)
+        flip_split(3, (scalar_copy, vector_copy))
+        transpose_unit(1)
+        quantise_a(0, 0, 4)
+        mix_bank(1, 0, vector_copy)
+        mix_bank(1, 1, vector_copy)
+        transpose_tile(2, 0, scalar_copy)
+        transpose_tile(2, 1, scalar_copy)
+        mix_on_vector(3)
+        mix_bank(1, 2, vector_copy)
+        mix_bank(1, 3, vector_copy)
+        transpose_tile(2, 2, scalar_copy)
+        transpose_tile(2, 3, scalar_copy)
+        quantise_unit(1)
+        quantise_a(1, 0, 4)
+        quantise_a(0, 4, 2)
+        quantise_a(1, 4, 2)
 
-        for first_step in range(PASSES, N_UNITS + MULTIPLY_LAG, ROUND_UNITS):
-            steps = range(first_step, first_step + ROUND_UNITS)
-            for step in steps:
-                if step + PREFETCH - PASSES < N_UNITS:
-                    load_unit(step + PREFETCH - PASSES)
-                if step < N_UNITS:
-                    transpose_unit(step)
-            for step in steps:
-                if step - PASSES < VECTOR_MIX_STEPS:
-                    mix_on_vector(
-                        PASSES * TERMS_BESIDE_A_PASS + (step - PASSES) * TERMS_BESIDE_A_UNIT, TERMS_BESIDE_A_UNIT
-                    )
-                if step <= N_UNITS:
-                    quantise_unit(step - 1)
-                if step - PASSES == VECTOR_MIX_STEPS:
-                    round_vector_mix()
-                    quantise_a_pair(TENSOR_EXAMPLES // 2)
-            for step in steps:
-                multiply_unit(step - MULTIPLY_LAG)
+        done = 0
+        loaded = X_BUFS
+        for first in range(3, N_UNITS + 1, 2):
+            units = range(first, min(first + 2, N_UNITS))
+            for i in units:
+                transpose_unit(i, (1, 3) if i == 15 else ())
+            for i in range(first - 1, min(first + 1, N_UNITS)):
+                mix_on_vector(5)
+                quantise_unit(i, 2 if i >= N_UNITS - 2 else 1)
+            if first == 11:
+                mix_on_vector(len(terms))
+                round_vector_mix()
+                for g in range(PASSES):
+                    quantise_a(g, 6, 2)
+            for i in range(done, min(done + 3, first - 1, N_UNITS)):
+                multiply_unit(i, scalar_copy)
+                done += 1
+                if loaded < N_UNITS and loaded - X_BUFS < first:
+                    load_unit(loaded)
+                    loaded += 1
+        for i in range(done, N_UNITS):
+            multiply_unit(i, vector_copy if i % 2 == 1 else scalar_copy)

@@ -92,13 +92,19 @@ def tile_skilledlora_pa_t_kernel(tc, x, weights, lora_a, out):
         )
 
         la_t = consts.tile([P, Q, C, P], BF16)
+        la_grouped = consts.tile([P, Q, C, P], BF16)
+
+        def regroup_split(q):
+            nc.vector.tensor_copy(
+                out=la_grouped[:, q].rearrange("p c (m r) -> p c m r", r=LANE_RANKS),
+                in_=la_sb[:, q].rearrange("p (m c r) -> p c m r", c=C, r=LANE_RANKS),
+            )
 
         def flip_split(q, engines):
-            la_lanes = la_sb[:, q].rearrange("p (m c) -> p m c", c=C)
             for half in range(2):
                 flipped = psum_work.tile([P, C // 2, P], BF16, tag="work")
                 for k in range(C // 2):
-                    nc.tensor.transpose(flipped[:, k, :], la_lanes[:, :, half * C // 2 + k], ident_bf16[:])
+                    nc.tensor.transpose(flipped[:, k, :], la_grouped[:, q, half * C // 2 + k, :], ident_bf16[:])
                 engines[half](out=la_t[:, q, half * C // 2 : (half + 1) * C // 2, :], in_=flipped[:])
 
         def tensor_examples(q):
@@ -130,37 +136,36 @@ def tile_skilledlora_pa_t_kernel(tc, x, weights, lora_a, out):
                 )
 
         a_grouped = consts.tile([P, PASSES * B * R * PACK], BF16, align_bytes=64)
-        a_grouped_runs = a_grouped[:].rearrange("p (g k c) -> p g k c", g=PASSES, c=C * PACK)
+        a_grouped_runs = a_grouped[:].rearrange("p (g b c) -> p g b c", g=PASSES, b=B)
         a_grouped_view = a_grouped[:].rearrange("p (g b r t) -> p b g r t", g=PASSES, b=B, t=PACK)
         a_codes = consts.tile([P, PASSES * B * R], U32, align_bytes=64)
         a_scales = consts.tile([P, PASSES * B * R], U8, align_bytes=64)
-        KT = TENSOR_EXAMPLES * LANE_RANKS
 
         def mix_bank(g, bank, copy):
             mixed = psum_work.tile([P, (TENSOR_EXAMPLES + 1) * LANE_RANKS * C_BANK * PACK], BF16, tag="work")
-            mixed_view = mixed[:].rearrange("p (k c u e) -> p k c u e", c=C_BANK, u=2, e=2)
+            mixed_view = mixed[:].rearrange("p (b c r u e) -> p b c r u e", c=C_BANK, r=LANE_RANKS, u=2, e=2)
             for c in range(C_BANK):
                 for u in range(2):
                     q = 2 * g + u
                     n = tensor_examples(q)
                     nc.tensor.matmul(
-                        out=mixed_view[:, 0 : n * LANE_RANKS, c, u, :],
+                        out=mixed_view[:, 0:n, c, :, u, :],
                         lhsT=la_t[:, q, bank * C_BANK + c, :],
-                        rhs=w_block[:, q, 0:n].rearrange("p b (r e) -> p (b r) e", e=2),
+                        rhs=w_block[:, q, 0:n].rearrange("p b (r e) -> p b r e", e=2),
                         start=True,
                         stop=True,
                     )
-            run = C_BANK * PACK
+            run = C_BANK * LANE_RANKS * PACK
             copy(
-                out=a_grouped_runs[:, g, 0:KT, bank * run : (bank + 1) * run],
-                in_=mixed[:].rearrange("p (k c) -> p k c", c=run)[:, 0:KT],
+                out=a_grouped_runs[:, g, 0:TENSOR_EXAMPLES, bank * run : (bank + 1) * run],
+                in_=mixed[:].rearrange("p (b c) -> p b c", c=run)[:, 0:TENSOR_EXAMPLES],
             )
             if g == 0:
                 nc.scalar.copy(
-                    out=mix_sums[TENSOR_EXAMPLES][:, 0 : 2 * R].rearrange("p (e r c) -> p e r c", e=2, c=C)[
-                        :, :, :, bank * C_BANK : (bank + 1) * C_BANK
+                    out=mix_sums[TENSOR_EXAMPLES][:, 0 : 2 * R].rearrange("p (e c r) -> p e c r", e=2, c=C)[
+                        :, :, bank * C_BANK : (bank + 1) * C_BANK
                     ],
-                    in_=mixed_view[:, KT : KT + LANE_RANKS, :, 0, :].rearrange("p r c e -> p e r c"),
+                    in_=mixed_view[:, TENSOR_EXAMPLES, :, :, 0, :].rearrange("p c r e -> p e c r"),
                 )
 
         mix_sums = {}
@@ -251,17 +256,21 @@ def tile_skilledlora_pa_t_kernel(tc, x, weights, lora_a, out):
             nc.sync.dma_start(out=out_units[b, h], in_=result[:])
 
         turn_weights()
+        regroup_split(0)
         flip_split(0, (scalar_copy, vector_copy))
+        regroup_split(1)
         spread_weights()
         flip_split(1, (scalar_copy, vector_copy))
         mix_on_vector(5)
         transpose_unit(0)
         mix_bank(0, 0, vector_copy)
         mix_bank(0, 1, vector_copy)
+        regroup_split(2)
         flip_split(2, (scalar_copy, vector_copy))
         mix_bank(0, 2, vector_copy)
         mix_bank(0, 3, vector_copy)
         quantise_unit(0)
+        regroup_split(3)
         flip_split(3, (scalar_copy, vector_copy))
         transpose_unit(1)
         quantise_a(0, 0, 4)

@@ -24,7 +24,7 @@ C = 16
 C_BANK = 4
 TENSOR_EXAMPLES = 6
 VECTOR_EXAMPLES = (6, 7)
-X_BUFS = 10
+X_BUFS = 9
 
 FLOPS = 2 * B * S * IN * R + 2 * B * IN * R * NS
 
@@ -40,7 +40,7 @@ def tile_skilledlora_pa_t_kernel(tc, x, weights, lora_a, out):
         x_pool = pools.enter_context(tc.tile_pool(name="x", bufs=X_BUFS))
         grouped_pool = pools.enter_context(tc.tile_pool(name="grouped", bufs=4))
         codes_pool = pools.enter_context(tc.tile_pool(name="codes", bufs=6))
-        out_pool = pools.enter_context(tc.tile_pool(name="outs", bufs=6))
+        out_pool = pools.enter_context(tc.tile_pool(name="outs", bufs=9))
         psum_work = pools.enter_context(tc.psum_pool(name="psum_work", bufs=6))
         psum_acc = pools.enter_context(tc.psum_pool(name="psum_acc", bufs=2))
         pools.enter_context(tc.manual_schedule())
@@ -257,33 +257,36 @@ def tile_skilledlora_pa_t_kernel(tc, x, weights, lora_a, out):
 
         turn_weights()
         regroup_split(0)
-        flip_split(0, (scalar_copy, vector_copy))
         regroup_split(1)
         spread_weights()
-        flip_split(1, (scalar_copy, vector_copy))
-        mix_on_vector(5)
-        transpose_unit(0)
+        flip_split(0, (scalar_copy, scalar_copy))
+        flip_split(1, (vector_copy, scalar_copy))
+        mix_on_vector(3)
         mix_bank(0, 0, vector_copy)
-        mix_bank(0, 1, vector_copy)
+        transpose_tile(0, 0, scalar_copy)
+        transpose_tile(0, 1, scalar_copy)
         regroup_split(2)
-        flip_split(2, (scalar_copy, vector_copy))
+        mix_bank(0, 1, vector_copy)
         mix_bank(0, 2, vector_copy)
-        mix_bank(0, 3, vector_copy)
-        quantise_unit(0)
+        transpose_tile(0, 2, scalar_copy)
+        transpose_tile(0, 3, scalar_copy)
         regroup_split(3)
+        flip_split(2, (scalar_copy, vector_copy))
+        mix_bank(0, 3, vector_copy)
         flip_split(3, (scalar_copy, vector_copy))
         transpose_unit(1)
-        quantise_a(0, 0, 4)
+        quantise_unit(0)
         mix_bank(1, 0, vector_copy)
         mix_bank(1, 1, vector_copy)
         transpose_tile(2, 0, scalar_copy)
         transpose_tile(2, 1, scalar_copy)
-        mix_on_vector(3)
+        quantise_a(0, 0, 4)
         mix_bank(1, 2, vector_copy)
         mix_bank(1, 3, vector_copy)
         transpose_tile(2, 2, scalar_copy)
         transpose_tile(2, 3, scalar_copy)
         quantise_unit(1)
+        mix_on_vector(3)
         quantise_a(1, 0, 4)
         quantise_a(0, 4, 2)
         quantise_a(1, 4, 2)

@@ -57,7 +57,7 @@ def tile_skilledlora_pa_t_kernel(tc, x, weights, lora_a, out):
 
         def load_unit(i):
             b, h = divmod(i, UNITS_PER_EXAMPLE)
-            x_sb = x_pool.tile([P, UNIT_TILES * IN], BF16)
+            x_sb = x_pool.tile([P, UNIT_TILES * IN], BF16, tag="x")
             nc.sync.dma_start(out=x_sb[:], in_=x_units[b, h])
             x_tiles[i] = x_sb
 
@@ -223,8 +223,8 @@ def tile_skilledlora_pa_t_kernel(tc, x, weights, lora_a, out):
                 transpose_tile(i, j, vector_copy if j in vector_tiles else scalar_copy)
 
         def quantise_unit(i, parts=1):
-            x_codes = codes_pool.tile([P, UNIT_TILES * PASSES * P], U32, align_bytes=64)
-            x_scales = codes_pool.tile([P, UNIT_TILES * PASSES * P], U8, align_bytes=64)
+            x_codes = codes_pool.tile([P, UNIT_TILES * PASSES * P], U32, align_bytes=64, tag="x_codes")
+            x_scales = codes_pool.tile([P, UNIT_TILES * PASSES * P], U8, align_bytes=64, tag="x_scales")
             code_tiles[i] = (x_codes, x_scales)
             words = UNIT_TILES * PASSES * P // parts
             for c in range(parts):
@@ -234,10 +234,23 @@ def tile_skilledlora_pa_t_kernel(tc, x, weights, lora_a, out):
                     in_=grouped_tiles[i][:, c * words * PACK : (c + 1) * words * PACK],
                 )
 
+        def quantise_half(i, c):
+            if c == 0:
+                x_codes = codes_pool.tile([P, UNIT_TILES * PASSES * P], U32, align_bytes=64, tag="x_codes")
+                x_scales = codes_pool.tile([P, UNIT_TILES * PASSES * P], U8, align_bytes=64, tag="x_scales")
+                code_tiles[i] = (x_codes, x_scales)
+            x_codes, x_scales = code_tiles[i]
+            words = UNIT_TILES * PASSES * P // 2
+            nc.vector.quantize_mx(
+                out=x_codes[:, c * words : (c + 1) * words].bitcast(FP8X4),
+                scales=x_scales[:, c * words : (c + 1) * words],
+                in_=grouped_tiles[i][:, c * words * PACK : (c + 1) * words * PACK],
+            )
+
         def multiply_unit(i, copy):
             b, h = divmod(i, UNITS_PER_EXAMPLE)
             x_codes, x_scales = code_tiles[i]
-            acc = psum_acc.tile([P, UNIT_TILES, R], F32)
+            acc = psum_acc.tile([P, UNIT_TILES, R], F32, tag="acc")
             for j in range(UNIT_TILES):
                 for g in range(PASSES):
                     x_cols = slice((j * PASSES + g) * P, (j * PASSES + g + 1) * P)
@@ -251,7 +264,7 @@ def tile_skilledlora_pa_t_kernel(tc, x, weights, lora_a, out):
                         start=(g == 0),
                         stop=(g == PASSES - 1),
                     )
-            result = out_pool.tile([P, UNIT_TILES * R], F32)
+            result = out_pool.tile([P, UNIT_TILES * R], F32, tag="whole")
             copy(out=result[:], in_=acc[:].rearrange("p j r -> p (j r)"))
             nc.sync.dma_start(out=out_units[b, h], in_=result[:])
 
@@ -260,24 +273,37 @@ def tile_skilledlora_pa_t_kernel(tc, x, weights, lora_a, out):
         regroup_split(1)
         spread_weights()
         flip_split(0, (scalar_copy, scalar_copy))
-        flip_split(1, (vector_copy, scalar_copy))
         mix_on_vector(3)
+        flip_split(1, (scalar_copy, scalar_copy))
+        mix_on_vector(4)
         mix_bank(0, 0, vector_copy)
+        mix_on_vector(1)
         transpose_tile(0, 0, scalar_copy)
         transpose_tile(0, 1, scalar_copy)
         regroup_split(2)
         mix_bank(0, 1, vector_copy)
+        mix_on_vector(1)
         mix_bank(0, 2, vector_copy)
+        mix_on_vector(1)
         transpose_tile(0, 2, scalar_copy)
         transpose_tile(0, 3, scalar_copy)
         regroup_split(3)
-        flip_split(2, (scalar_copy, vector_copy))
+        mix_on_vector(1)
+        flip_split(2, (scalar_copy, scalar_copy))
+        mix_on_vector(1)
         mix_bank(0, 3, vector_copy)
+        mix_on_vector(1)
         flip_split(3, (scalar_copy, vector_copy))
-        transpose_unit(1)
+        mix_on_vector(1)
+        transpose_tile(1, 0, scalar_copy)
+        transpose_tile(1, 1, scalar_copy)
+        transpose_tile(1, 2, scalar_copy)
+        transpose_tile(1, 3, scalar_copy)
         quantise_unit(0)
         mix_bank(1, 0, vector_copy)
+        mix_on_vector(1)
         mix_bank(1, 1, vector_copy)
+        mix_on_vector(1)
         transpose_tile(2, 0, scalar_copy)
         transpose_tile(2, 1, scalar_copy)
         quantise_a(0, 0, 4)
@@ -286,30 +312,29 @@ def tile_skilledlora_pa_t_kernel(tc, x, weights, lora_a, out):
         transpose_tile(2, 2, scalar_copy)
         transpose_tile(2, 3, scalar_copy)
         quantise_unit(1)
-        mix_on_vector(3)
+        mix_on_vector(2)
         quantise_a(1, 0, 4)
         quantise_a(0, 4, 2)
         quantise_a(1, 4, 2)
 
-        done = 0
         loaded = X_BUFS
-        for first in range(3, N_UNITS + 1, 2):
-            units = range(first, min(first + 2, N_UNITS))
+        for units, ready, products in [[[3,4],[[2,-1],[3,-1]],[0,1]],[[5,6],[[4,-1],[5,-1]],[2,3]],[[7,8],[[6,-1],[7,-1]],[4,5]],[[9,10],[[8,-1],[9,-1]],[6,7]],[[11,12],[[10,-1],[11,-1]],[8,9]],[[13,14],[[12,-1],[13,-1]],[10,11]],[[15],[[14,0],[14,1],[15,0],[15,1]],[12,13]],[[],[],[14,15]]]:
             for i in units:
-                transpose_unit(i, (1, 3) if i == 15 else ())
-            for i in range(first - 1, min(first + 1, N_UNITS)):
-                mix_on_vector(5)
-                quantise_unit(i, 2 if i >= N_UNITS - 2 else 1)
-            if first == 11:
+                transpose_unit(i, ())
+                if loaded < min(N_UNITS, i + 1 + X_BUFS):
+                    load_unit(loaded)
+                    loaded += 1
+            for i, c in ready:
+                if c <= 0:
+                    mix_on_vector(4)
+                if c < 0:
+                    quantise_unit(i)
+                else:
+                    quantise_half(i, c)
+            if 13 in units:
                 mix_on_vector(len(terms))
                 round_vector_mix()
                 for g in range(PASSES):
                     quantise_a(g, 6, 2)
-            for i in range(done, min(done + 3, first - 1, N_UNITS)):
-                multiply_unit(i, scalar_copy)
-                done += 1
-                if loaded < N_UNITS and loaded - X_BUFS < first:
-                    load_unit(loaded)
-                    loaded += 1
-        for i in range(done, N_UNITS):
-            multiply_unit(i, vector_copy if i % 2 == 1 else scalar_copy)
+            for i in products:
+                multiply_unit(i, vector_copy if i % 4 == 3 else scalar_copy)

@@ -50,8 +50,6 @@ def tile_skilledlora_pa_t_kernel(tc, x, weights, lora_a, out):
 
         w_rows = consts.tile([P, NS], BF16)
         nc.gpsimd.memset(w_rows[:], 0.0)
-        w_line = consts.tile([P, len(VECTOR_EXAMPLES) * Q * NS], BF16)
-        nc.gpsimd.memset(w_line[:], 0.0)
         la_sb = consts.tile([P, Q, NS * 2 * R], BF16)
         x_tiles = {}
 
@@ -65,10 +63,6 @@ def tile_skilledlora_pa_t_kernel(tc, x, weights, lora_a, out):
             nc.sync.dma_start(out=la_sb[:, q].rearrange("p (s c) -> p s c", s=NS), in_=la_splits[q])
 
         nc.sync.dma_start(out=w_rows[0 : B * Q, :], in_=weights.rearrange("b q s -> (b q) s"))
-        nc.sync.dma_start(
-            out=w_line[0:1, :],
-            in_=weights[VECTOR_EXAMPLES[0] : B].rearrange("(o b) q s -> o (b q s)", o=1),
-        )
         load_split(0)
         load_split(1)
         load_unit(0)
@@ -81,8 +75,6 @@ def tile_skilledlora_pa_t_kernel(tc, x, weights, lora_a, out):
         make_identity(nc, ident_f32[:])
         ident_bf16 = consts.tile([P, P], BF16)
         make_identity(nc, ident_bf16[:])
-        ones = consts.tile([P, P], BF16)
-        nc.vector.memset(ones[:], 1.0)
         lane_of_row = consts.tile([P, J], F32)
         nc.vector.tensor_reduce(
             out=lane_of_row[:].rearrange("p (r e) -> p r e", e=2),
@@ -107,12 +99,14 @@ def tile_skilledlora_pa_t_kernel(tc, x, weights, lora_a, out):
                     nc.tensor.transpose(flipped[:, k, :], la_grouped[:, q, half * C // 2 + k, :], ident_bf16[:])
                 engines[half](out=la_t[:, q, half * C // 2 : (half + 1) * C // 2, :], in_=flipped[:])
 
-        def tensor_examples(q):
-            return TENSOR_EXAMPLES + 1 if q == 0 else TENSOR_EXAMPLES
+        def tensor_examples(q, bank):
+            if q > 0:
+                return TENSOR_EXAMPLES
+            return TENSOR_EXAMPLES + 2 if bank < C // C_BANK // 2 else TENSOR_EXAMPLES + 1
 
         w_rep = consts.tile([P, NS, J], BF16)
         w_row = consts.tile([P, B * Q], F32)
-        w_block = consts.tile([P, Q, TENSOR_EXAMPLES + 1, J], BF16)
+        w_block = consts.tile([P, Q, B, J], BF16)
         w_f32 = consts.tile([P, len(VECTOR_EXAMPLES), Q, NS], F32)
 
         def turn_weights():
@@ -121,13 +115,17 @@ def tile_skilledlora_pa_t_kernel(tc, x, weights, lora_a, out):
         def spread_weights():
             w_turned = psum_work.tile([P, P], BF16, tag="work")
             nc.tensor.transpose(w_turned[:], w_rep[:].rearrange("p s j -> p (s j)"), ident_bf16[:])
-            w_spread = psum_work.tile([P, len(VECTOR_EXAMPLES) * Q * NS], F32, tag="work")
-            nc.tensor.matmul(out=w_spread[:], lhsT=ones[:], rhs=w_line[:], start=True, stop=True)
+            w_spread = psum_work.tile([P, NS, P], BF16, tag="work")
+            for s in range(NS):
+                nc.tensor.transpose(w_spread[:, s, :], w_rows[:, s : s + 1].to_broadcast([P, P]), ident_bf16[:])
             nc.vector.tensor_copy(out=w_row[:], in_=w_turned[:, 0 : B * Q])
-            nc.vector.tensor_copy(out=w_f32[:].rearrange("p b q s -> p (b q s)"), in_=w_spread[:])
+            nc.vector.tensor_copy(
+                out=w_f32[:].rearrange("p b q s -> p (b q) s"),
+                in_=w_spread[:, :, VECTOR_EXAMPLES[0] * Q : B * Q].rearrange("p s k -> p k s"),
+            )
             w_row_view = w_row[:].rearrange("p (b q) -> p b q", q=Q)
             for q in range(Q):
-                n = tensor_examples(q)
+                n = tensor_examples(q, 0)
                 nc.vector.tensor_tensor(
                     out=w_block[:, q, 0:n],
                     in0=lane_of_row[:].unsqueeze(1).to_broadcast([P, n, J]),
@@ -142,12 +140,12 @@ def tile_skilledlora_pa_t_kernel(tc, x, weights, lora_a, out):
         a_scales = consts.tile([P, PASSES * B * R], U8, align_bytes=64)
 
         def mix_bank(g, bank, copy):
-            mixed = psum_work.tile([P, (TENSOR_EXAMPLES + 1) * LANE_RANKS * C_BANK * PACK], BF16, tag="work")
+            mixed = psum_work.tile([P, B * LANE_RANKS * C_BANK * PACK], BF16, tag="work")
             mixed_view = mixed[:].rearrange("p (b c r u e) -> p b c r u e", c=C_BANK, r=LANE_RANKS, u=2, e=2)
             for c in range(C_BANK):
                 for u in range(2):
                     q = 2 * g + u
-                    n = tensor_examples(q)
+                    n = tensor_examples(q, bank)
                     nc.tensor.matmul(
                         out=mixed_view[:, 0:n, c, :, u, :],
                         lhsT=la_t[:, q, bank * C_BANK + c, :],
@@ -161,39 +159,35 @@ def tile_skilledlora_pa_t_kernel(tc, x, weights, lora_a, out):
                 in_=mixed[:].rearrange("p (b c) -> p b c", c=run)[:, 0:TENSOR_EXAMPLES],
             )
             if g == 0:
+                n = tensor_examples(0, bank) - TENSOR_EXAMPLES
+                ranks = slice(bank * C_BANK * LANE_RANKS, (bank + 1) * C_BANK * LANE_RANKS)
                 nc.scalar.copy(
-                    out=mix_sums[TENSOR_EXAMPLES][:, 0 : 2 * R].rearrange("p (e c r) -> p e c r", e=2, c=C)[
-                        :, :, bank * C_BANK : (bank + 1) * C_BANK
-                    ],
-                    in_=mixed_view[:, TENSOR_EXAMPLES, :, :, 0, :].rearrange("p c r e -> p e c r"),
+                    out=mix_sums[:, 0:n, 0 : 2 * R].rearrange("p b (e r) -> p b e r", e=2)[:, :, :, ranks],
+                    in_=mixed_view[:, TENSOR_EXAMPLES : TENSOR_EXAMPLES + n, :, :, 0, :].rearrange("p b c r e -> p b e (c r)"),
                 )
 
-        mix_sums = {}
-        for b in VECTOR_EXAMPLES:
-            mix_sum = consts.tile([P, Q * 2 * R], F32, name="mix_sum%d" % b)
-            mix_sums[b] = mix_sum
+        mix_sums = consts.tile([P, len(VECTOR_EXAMPLES), Q * 2 * R], F32)
         terms = [(b, q, s) for s in range(NS) for b, q in ((7, 0), (6, 1), (7, 1))]
         terms += [(b, q, s) for q in (2, 3) for s in range(NS) for b in VECTOR_EXAMPLES]
 
         def mix_on_vector(count):
             for k in range(min(count, len(terms))):
                 b, q, s = terms.pop(0)
-                cols = slice(q * 2 * R, (q + 1) * 2 * R)
-                la = la_sb[:, q, s * 2 * R : (s + 1) * 2 * R]
+                ranks = slice(R // 2 if q == 0 else 0, R)
+                total = mix_sums[:, b - VECTOR_EXAMPLES[0], q * 2 * R : (q + 1) * 2 * R]
+                total = total.rearrange("p (e r) -> p e r", e=2)[:, :, ranks]
+                la = la_sb[:, q, s * 2 * R : (s + 1) * 2 * R].rearrange("p (e r) -> p e r", e=2)[:, :, ranks]
                 w = w_f32[:, b - VECTOR_EXAMPLES[0], q, s : s + 1]
                 if s == 0:
-                    nc.vector.tensor_scalar_mul(out=mix_sums[b][:, cols], in0=la, scalar1=w)
+                    nc.vector.tensor_scalar_mul(out=total, in0=la, scalar1=w)
                 else:
-                    nc.vector.scalar_tensor_tensor(
-                        out=mix_sums[b][:, cols], in0=la, scalar=w, in1=mix_sums[b][:, cols],
-                        op0=ALU.mult, op1=ALU.add,
-                    )
+                    nc.vector.scalar_tensor_tensor(out=total, in0=la, scalar=w, in1=total, op0=ALU.mult, op1=ALU.add)
 
         def round_vector_mix():
             for b in VECTOR_EXAMPLES:
                 nc.vector.tensor_copy(
                     out=a_grouped_view[:, b],
-                    in_=mix_sums[b][:].rearrange("p (g t r) -> p g r t", g=PASSES, t=PACK),
+                    in_=mix_sums[:, b - VECTOR_EXAMPLES[0]].rearrange("p (g t r) -> p g r t", g=PASSES, t=PACK),
                 )
 
         def quantise_a(g, first, count):

@@ -212,45 +212,35 @@ def tile_skilledlora_pa_t_kernel(tc, x, weights, lora_a, out):
                 nc.tensor.transpose(flipped_x[:, q, :], x_words[:, first : first + P], ident_f32[:])
             copy(out=grouped_words[:, j], in_=flipped_x[:].rearrange("p (g u) r -> p g r u", u=2))
 
-        def transpose_unit(i, vector_tiles=()):
+        def transpose_unit(i):
             for j in range(UNIT_TILES):
-                transpose_tile(i, j, vector_copy if j in vector_tiles else scalar_copy)
+                transpose_tile(i, j, scalar_copy)
 
-        def quantise_unit(i, parts=1):
-            x_codes = codes_pool.tile([P, UNIT_TILES * PASSES * P], U32, align_bytes=64, tag="x_codes")
-            x_scales = codes_pool.tile([P, UNIT_TILES * PASSES * P], U8, align_bytes=64, tag="x_scales")
-            code_tiles[i] = (x_codes, x_scales)
-            words = UNIT_TILES * PASSES * P // parts
-            for c in range(parts):
-                nc.vector.quantize_mx(
-                    out=x_codes[:, c * words : (c + 1) * words].bitcast(FP8X4),
-                    scales=x_scales[:, c * words : (c + 1) * words],
-                    in_=grouped_tiles[i][:, c * words * PACK : (c + 1) * words * PACK],
-                )
-
-        def quantise_half(i, c):
-            if c == 0:
+        def quantise_tiles(i, first, count):
+            if first == 0:
                 x_codes = codes_pool.tile([P, UNIT_TILES * PASSES * P], U32, align_bytes=64, tag="x_codes")
                 x_scales = codes_pool.tile([P, UNIT_TILES * PASSES * P], U8, align_bytes=64, tag="x_scales")
                 code_tiles[i] = (x_codes, x_scales)
             x_codes, x_scales = code_tiles[i]
-            words = UNIT_TILES * PASSES * P // 2
-            nc.vector.quantize_mx(
-                out=x_codes[:, c * words : (c + 1) * words].bitcast(FP8X4),
-                scales=x_scales[:, c * words : (c + 1) * words],
-                in_=grouped_tiles[i][:, c * words * PACK : (c + 1) * words * PACK],
-            )
+            words = slice(first * PASSES * P, (first + count) * PASSES * P)
+            values = slice(first * IN, (first + count) * IN)
+            nc.vector.quantize_mx(out=x_codes[:, words].bitcast(FP8X4), scales=x_scales[:, words], in_=grouped_tiles[i][:, values])
 
-        def multiply_unit(i, copy):
+        def quantise_unit(i):
+            quantise_tiles(i, 0, UNIT_TILES)
+
+        results = {}
+
+        def multiply_tiles(i, first, count, copy, pool=psum_acc, tag="acc"):
             b, h = divmod(i, UNITS_PER_EXAMPLE)
             x_codes, x_scales = code_tiles[i]
-            acc = psum_acc.tile([P, UNIT_TILES, R], F32, tag="acc")
-            for j in range(UNIT_TILES):
+            acc = pool.tile([P, count, R], F32, tag=tag)
+            for j in range(first, first + count):
                 for g in range(PASSES):
                     x_cols = slice((j * PASSES + g) * P, (j * PASSES + g + 1) * P)
                     a_cols = slice((g * B + b) * R, (g * B + b + 1) * R)
                     nc.tensor.matmul_mx(
-                        out=acc[:, j, :],
+                        out=acc[:, j - first, :],
                         lhsT=x_codes[:, x_cols].bitcast(FP8X4),
                         lhsT_scale=x_scales[:, x_cols],
                         rhs=a_codes[:, a_cols].bitcast(FP8X4),
@@ -258,9 +248,16 @@ def tile_skilledlora_pa_t_kernel(tc, x, weights, lora_a, out):
                         start=(g == 0),
                         stop=(g == PASSES - 1),
                     )
-            result = out_pool.tile([P, UNIT_TILES * R], F32, tag="whole")
-            copy(out=result[:], in_=acc[:].rearrange("p j r -> p (j r)"))
-            nc.sync.dma_start(out=out_units[b, h], in_=result[:])
+            if first == 0:
+                result = out_pool.tile([P, UNIT_TILES * R], F32, tag="whole")
+                results[i] = result
+            cols = slice(first * R, (first + count) * R)
+            copy(out=results[i][:, cols], in_=acc[:].rearrange("p j r -> p (j r)"))
+            if first + count == UNIT_TILES:
+                nc.sync.dma_start(out=out_units[b, h], in_=results[i][:])
+
+        def multiply_unit(i, copy):
+            multiply_tiles(i, 0, UNIT_TILES, copy)
 
         turn_weights()
         regroup_split(0)
@@ -287,7 +284,7 @@ def tile_skilledlora_pa_t_kernel(tc, x, weights, lora_a, out):
         mix_on_vector(1)
         mix_bank(0, 3, vector_copy)
         mix_on_vector(1)
-        flip_split(3, (scalar_copy, vector_copy))
+        flip_split(3, (scalar_copy, scalar_copy))
         mix_on_vector(1)
         transpose_tile(1, 0, scalar_copy)
         transpose_tile(1, 1, scalar_copy)
@@ -312,23 +309,33 @@ def tile_skilledlora_pa_t_kernel(tc, x, weights, lora_a, out):
         quantise_a(1, 4, 2)
 
         loaded = X_BUFS
-        for units, ready, products in [[[3,4],[[2,-1],[3,-1]],[0,1]],[[5,6],[[4,-1],[5,-1]],[2,3]],[[7,8],[[6,-1],[7,-1]],[4,5]],[[9,10],[[8,-1],[9,-1]],[6,7]],[[11,12],[[10,-1],[11,-1]],[8,9]],[[13,14],[[12,-1],[13,-1]],[10,11]],[[15],[[14,0],[14,1],[15,0],[15,1]],[12,13]],[[],[],[14,15]]]:
-            for i in units:
-                transpose_unit(i, ())
-                if loaded < min(N_UNITS, i + 1 + X_BUFS):
+        for i in range(3, 13, 2):
+            for unit in (i, i + 1):
+                transpose_unit(unit)
+                if loaded < N_UNITS:
                     load_unit(loaded)
                     loaded += 1
-            for i, c in ready:
-                if c <= 0:
-                    mix_on_vector(4)
-                if c < 0:
-                    quantise_unit(i)
-                else:
-                    quantise_half(i, c)
-            if 13 in units:
+            for unit in (i - 1, i):
+                mix_on_vector(4)
+                quantise_unit(unit)
+            if i == 11:
                 mix_on_vector(len(terms))
                 round_vector_mix()
                 for g in range(PASSES):
                     quantise_a(g, 6, 2)
-            for i in products:
-                multiply_unit(i, vector_copy if i % 4 == 3 else scalar_copy)
+            for unit in (i - 3, i - 2):
+                multiply_unit(unit, vector_copy if unit % 4 == 3 else scalar_copy)
+        for i in range(13, N_UNITS):
+            transpose_tile(i, 0, scalar_copy)
+            transpose_tile(i, 1, vector_copy)
+            transpose_tile(i, 2, scalar_copy)
+            multiply_unit(i - 3, scalar_copy)
+            transpose_tile(i, 3, scalar_copy)
+            quantise_unit(i - 1)
+        multiply_unit(N_UNITS - 3, scalar_copy)
+        last = N_UNITS - 1
+        for j in range(UNIT_TILES):
+            quantise_tiles(last, j, 1)
+        multiply_unit(last - 1, vector_copy)
+        multiply_tiles(last, 0, 2, scalar_copy)
+        multiply_tiles(last, 2, 2, scalar_copy, psum_work, "work")

@@ -32,7 +32,7 @@ FLOPS = 2 * B * S * IN * R + 2 * B * IN * R * NS
 def tile_skilledlora_pa_t_kernel(tc, x, weights, lora_a, out):
     nc = tc.nc
     x_units = x.rearrange("b (p h j) k -> b h p (j k)", h=UNITS_PER_EXAMPLE, j=UNIT_TILES)
-    out_units = out.rearrange("b (p h j) r -> b h p (j r)", h=UNITS_PER_EXAMPLE, j=UNIT_TILES)
+    out_rows = out.rearrange("b (p t) r -> b p (t r)", p=P)
     la_splits = lora_a.rearrange("q s (p e) r -> q p s (e r)", e=2)
 
     with ExitStack() as pools:
@@ -40,7 +40,7 @@ def tile_skilledlora_pa_t_kernel(tc, x, weights, lora_a, out):
         x_pool = pools.enter_context(tc.tile_pool(name="x", bufs=X_BUFS))
         grouped_pool = pools.enter_context(tc.tile_pool(name="grouped", bufs=4))
         codes_pool = pools.enter_context(tc.tile_pool(name="codes", bufs=6))
-        out_pool = pools.enter_context(tc.tile_pool(name="outs", bufs=9))
+        out_pool = pools.enter_context(tc.tile_pool(name="outs", bufs=5))
         psum_work = pools.enter_context(tc.psum_pool(name="psum_work", bufs=6))
         psum_acc = pools.enter_context(tc.psum_pool(name="psum_acc", bufs=2))
         pools.enter_context(tc.manual_schedule())
@@ -248,13 +248,14 @@ def tile_skilledlora_pa_t_kernel(tc, x, weights, lora_a, out):
                         start=(g == 0),
                         stop=(g == PASSES - 1),
                     )
-            if first == 0:
-                result = out_pool.tile([P, UNIT_TILES * R], F32, tag="whole")
-                results[i] = result
-            cols = slice(first * R, (first + count) * R)
-            copy(out=results[i][:, cols], in_=acc[:].rearrange("p j r -> p (j r)"))
-            if first + count == UNIT_TILES:
-                nc.sync.dma_start(out=out_units[b, h], in_=results[i][:])
+            if h == 0 and first == 0:
+                result = out_pool.tile([P, UNITS_PER_EXAMPLE * UNIT_TILES * R], F32, tag="whole")
+                results[b] = result
+            start = h * UNIT_TILES + first
+            copy(out=results[b][:, start * R : (start + count) * R], in_=acc[:].rearrange("p j r -> p (j r)"))
+            if first + count == UNIT_TILES and (h == UNITS_PER_EXAMPLE - 1 or b == B - 1):
+                cols = slice(h * UNIT_TILES * R if b == B - 1 else 0, (h + 1) * UNIT_TILES * R)
+                nc.sync.dma_start(out=out_rows[b][:, cols], in_=results[b][:, cols])
 
         def multiply_unit(i, copy):
             multiply_tiles(i, 0, UNIT_TILES, copy)
@@ -278,6 +279,7 @@ def tile_skilledlora_pa_t_kernel(tc, x, weights, lora_a, out):
         mix_on_vector(1)
         transpose_tile(0, 2, scalar_copy)
         transpose_tile(0, 3, scalar_copy)
+        load_unit(X_BUFS)
         regroup_split(3)
         mix_on_vector(1)
         flip_split(2, (scalar_copy, scalar_copy))
@@ -290,6 +292,7 @@ def tile_skilledlora_pa_t_kernel(tc, x, weights, lora_a, out):
         transpose_tile(1, 1, scalar_copy)
         transpose_tile(1, 2, scalar_copy)
         transpose_tile(1, 3, scalar_copy)
+        load_unit(1 + X_BUFS)
         quantise_unit(0)
         mix_bank(1, 0, vector_copy)
         mix_on_vector(1)
@@ -302,19 +305,18 @@ def tile_skilledlora_pa_t_kernel(tc, x, weights, lora_a, out):
         mix_bank(1, 3, vector_copy)
         transpose_tile(2, 2, scalar_copy)
         transpose_tile(2, 3, scalar_copy)
+        load_unit(2 + X_BUFS)
         quantise_unit(1)
         mix_on_vector(2)
         quantise_a(1, 0, 4)
         quantise_a(0, 4, 2)
         quantise_a(1, 4, 2)
 
-        loaded = X_BUFS
         for i in range(3, 13, 2):
             for unit in (i, i + 1):
                 transpose_unit(unit)
-                if loaded < N_UNITS:
-                    load_unit(loaded)
-                    loaded += 1
+                if unit + X_BUFS < N_UNITS:
+                    load_unit(unit + X_BUFS)
             for unit in (i - 1, i):
                 mix_on_vector(4)
                 quantise_unit(unit)

from contextlib import ExitStack

import concourse.mybir as mybir
from concourse.masks import make_identity

F32 = mybir.dt.float32
BF16 = mybir.dt.bfloat16
U32 = mybir.dt.uint32
U8 = mybir.dt.uint8
FP8X4 = mybir.dt.float8_e4m3fn_x4
ALU = mybir.AluOpType
AX = mybir.AxisListType

B, S, IN, Q, NS, R = 8, 1024, 1024, 4, 8, 128
P = 128
PACK = 4
PASSES = IN // (P * PACK)
UNIT_TILES = 4
UNITS_PER_EXAMPLE = S // (P * UNIT_TILES)
N_UNITS = B * UNITS_PER_EXAMPLE
J = P // NS
LANE_RANKS = J // 2
C = 16
C_BANK = 4
TENSOR_EXAMPLES = 6
VECTOR_EXAMPLES = (6, 7)
X_BUFS = 9

FLOPS = 2 * B * S * IN * R + 2 * B * IN * R * NS


def tile_skilledlora_pa_t_kernel(tc, x, weights, lora_a, out):
    nc = tc.nc
    x_units = x.rearrange("b (p h j) k -> b h p (j k)", h=UNITS_PER_EXAMPLE, j=UNIT_TILES)
    out_rows = out.rearrange("b (p t) r -> b p (t r)", p=P)
    la_splits = lora_a.rearrange("q s (p e) r -> q p s (e r)", e=2)

    with ExitStack() as pools:
        consts = pools.enter_context(tc.tile_pool(name="consts", bufs=1))
        x_pool = pools.enter_context(tc.tile_pool(name="x", bufs=X_BUFS))
        grouped_pool = pools.enter_context(tc.tile_pool(name="grouped", bufs=4))
        codes_pool = pools.enter_context(tc.tile_pool(name="codes", bufs=6))
        out_pool = pools.enter_context(tc.tile_pool(name="outs", bufs=5))
        psum_work = pools.enter_context(tc.psum_pool(name="psum_work", bufs=6))
        psum_acc = pools.enter_context(tc.psum_pool(name="psum_acc", bufs=2))
        pools.enter_context(tc.manual_schedule())

        scalar_copy = nc.scalar.copy
        vector_copy = nc.vector.tensor_copy

        w_rows = consts.tile([P, NS], BF16)
        nc.gpsimd.memset(w_rows[:], 0.0)
        la_sb = consts.tile([P, Q, NS * 2 * R], BF16)
        x_tiles = {}

        def load_unit(i):
            b, h = divmod(i, UNITS_PER_EXAMPLE)
            x_sb = x_pool.tile([P, UNIT_TILES * IN], BF16, tag="x")
            nc.sync.dma_start(out=x_sb[:], in_=x_units[b, h])
            x_tiles[i] = x_sb

        def load_split(q):
            nc.sync.dma_start(out=la_sb[:, q].rearrange("p (s c) -> p s c", s=NS), in_=la_splits[q])

        nc.sync.dma_start(out=w_rows[0 : B * Q, :], in_=weights.rearrange("b q s -> (b q) s"))
        load_split(0)
        load_split(1)
        load_unit(0)
        load_split(2)
        load_split(3)
        for i in range(1, X_BUFS):
            load_unit(i)

        ident_f32 = consts.tile([P, P], F32)
        make_identity(nc, ident_f32[:])
        ident_bf16 = consts.tile([P, P], BF16)
        make_identity(nc, ident_bf16[:])
        lane_of_row = consts.tile([P, J], F32)
        nc.vector.tensor_reduce(
            out=lane_of_row[:].rearrange("p (r e) -> p r e", e=2),
            in_=ident_f32[:].rearrange("p (s e r) -> p r e s", s=NS, e=2),
            axis=AX.X,
            op=ALU.add,
        )

        la_t = consts.tile([P, Q, C, P], BF16)
        la_grouped = consts.tile([P, Q, C, P], BF16)

        def regroup_split(q):
            nc.vector.tensor_copy(
                out=la_grouped[:, q].rearrange("p c (m r) -> p c m r", r=LANE_RANKS),
                in_=la_sb[:, q].rearrange("p (m c r) -> p c m r", c=C, r=LANE_RANKS),
            )

        def flip_split(q, engines):
            for half in range(2):
                flipped = psum_work.tile([P, C // 2, P], BF16, tag="work")
                for k in range(C // 2):
                    nc.tensor.transpose(flipped[:, k, :], la_grouped[:, q, half * C // 2 + k, :], ident_bf16[:])
                engines[half](out=la_t[:, q, half * C // 2 : (half + 1) * C // 2, :], in_=flipped[:])

        def tensor_examples(q, bank):
            if q > 0:
                return TENSOR_EXAMPLES
            return TENSOR_EXAMPLES + 2 if bank < C // C_BANK // 2 else TENSOR_EXAMPLES + 1

        w_rep = consts.tile([P, NS, J], BF16)
        w_row = consts.tile([P, B * Q], F32)
        w_block = consts.tile([P, Q, B, J], BF16)
        w_f32 = consts.tile([P, len(VECTOR_EXAMPLES), Q, NS], F32)

        def turn_weights():
            nc.vector.tensor_copy(out=w_rep[:], in_=w_rows[:].unsqueeze(2).to_broadcast([P, NS, J]))

        def spread_weights():
            w_turned = psum_work.tile([P, P], BF16, tag="work")
            nc.tensor.transpose(w_turned[:], w_rep[:].rearrange("p s j -> p (s j)"), ident_bf16[:])
            w_spread = psum_work.tile([P, NS, P], BF16, tag="work")
            for s in range(NS):
                nc.tensor.transpose(w_spread[:, s, :], w_rows[:, s : s + 1].to_broadcast([P, P]), ident_bf16[:])
            nc.vector.tensor_copy(out=w_row[:], in_=w_turned[:, 0 : B * Q])
            nc.vector.tensor_copy(
                out=w_f32[:].rearrange("p b q s -> p (b q) s"),
                in_=w_spread[:, :, VECTOR_EXAMPLES[0] * Q : B * Q].rearrange("p s k -> p k s"),
            )
            w_row_view = w_row[:].rearrange("p (b q) -> p b q", q=Q)
            for q in range(Q):
                n = tensor_examples(q, 0)
                nc.vector.tensor_tensor(
                    out=w_block[:, q, 0:n],
                    in0=lane_of_row[:].unsqueeze(1).to_broadcast([P, n, J]),
                    in1=w_row_view[:, 0:n, q].unsqueeze(2).to_broadcast([P, n, J]),
                    op=ALU.mult,
                )

        a_grouped = consts.tile([P, PASSES * B * R * PACK], BF16, align_bytes=64)
        a_grouped_runs = a_grouped[:].rearrange("p (g b c) -> p g b c", g=PASSES, b=B)
        a_grouped_view = a_grouped[:].rearrange("p (g b r t) -> p b g r t", g=PASSES, b=B, t=PACK)
        a_codes = consts.tile([P, PASSES * B * R], U32, align_bytes=64)
        a_scales = consts.tile([P, PASSES * B * R], U8, align_bytes=64)

        def mix_bank(g, bank, copy):
            mixed = psum_work.tile([P, B * LANE_RANKS * C_BANK * PACK], BF16, tag="work")
            mixed_view = mixed[:].rearrange("p (b c r u e) -> p b c r u e", c=C_BANK, r=LANE_RANKS, u=2, e=2)
            for c in range(C_BANK):
                for u in range(2):
                    q = 2 * g + u
                    n = tensor_examples(q, bank)
                    nc.tensor.matmul(
                        out=mixed_view[:, 0:n, c, :, u, :],
                        lhsT=la_t[:, q, bank * C_BANK + c, :],
                        rhs=w_block[:, q, 0:n].rearrange("p b (r e) -> p b r e", e=2),
                        start=True,
                        stop=True,
                    )
            run = C_BANK * LANE_RANKS * PACK
            copy(
                out=a_grouped_runs[:, g, 0:TENSOR_EXAMPLES, bank * run : (bank + 1) * run],
                in_=mixed[:].rearrange("p (b c) -> p b c", c=run)[:, 0:TENSOR_EXAMPLES],
            )
            if g == 0:
                n = tensor_examples(0, bank) - TENSOR_EXAMPLES
                ranks = slice(bank * C_BANK * LANE_RANKS, (bank + 1) * C_BANK * LANE_RANKS)
                nc.scalar.copy(
                    out=mix_sums[:, 0:n, 0 : 2 * R].rearrange("p b (e r) -> p b e r", e=2)[:, :, :, ranks],
                    in_=mixed_view[:, TENSOR_EXAMPLES : TENSOR_EXAMPLES + n, :, :, 0, :].rearrange("p b c r e -> p b e (c r)"),
                )

        mix_sums = consts.tile([P, len(VECTOR_EXAMPLES), Q * 2 * R], F32)
        terms = [(b, q, s) for s in range(NS) for b, q in ((7, 0), (6, 1), (7, 1))]
        terms += [(b, q, s) for q in (2, 3) for s in range(NS) for b in VECTOR_EXAMPLES]

        def mix_on_vector(count):
            for k in range(min(count, len(terms))):
                b, q, s = terms.pop(0)
                ranks = slice(R // 2 if q == 0 else 0, R)
                total = mix_sums[:, b - VECTOR_EXAMPLES[0], q * 2 * R : (q + 1) * 2 * R]
                total = total.rearrange("p (e r) -> p e r", e=2)[:, :, ranks]
                la = la_sb[:, q, s * 2 * R : (s + 1) * 2 * R].rearrange("p (e r) -> p e r", e=2)[:, :, ranks]
                w = w_f32[:, b - VECTOR_EXAMPLES[0], q, s : s + 1]
                if s == 0:
                    nc.vector.tensor_scalar_mul(out=total, in0=la, scalar1=w)
                else:
                    nc.vector.scalar_tensor_tensor(out=total, in0=la, scalar=w, in1=total, op0=ALU.mult, op1=ALU.add)

        def round_vector_mix():
            for b in VECTOR_EXAMPLES:
                nc.vector.tensor_copy(
                    out=a_grouped_view[:, b],
                    in_=mix_sums[:, b - VECTOR_EXAMPLES[0]].rearrange("p (g t r) -> p g r t", g=PASSES, t=PACK),
                )

        def quantise_a(g, first, count):
            cols = slice((g * B + first) * R, (g * B + first + count) * R)
            wide = slice((g * B + first) * R * PACK, (g * B + first + count) * R * PACK)
            nc.vector.quantize_mx(out=a_codes[:, cols].bitcast(FP8X4), scales=a_scales[:, cols], in_=a_grouped[:, wide])

        grouped_tiles = {}
        code_tiles = {}

        def transpose_tile(i, j, copy):
            if j == 0:
                x_grouped = grouped_pool.tile([P, UNIT_TILES * IN], BF16, align_bytes=64)
                grouped_tiles[i] = x_grouped
            x_words = x_tiles[i][:].bitcast(F32)
            grouped_words = grouped_tiles[i][:].bitcast(F32).rearrange(
                "p (j g r u) -> p j g r u", j=UNIT_TILES, g=PASSES, u=2
            )
            flipped_x = psum_work.tile([P, Q, P], F32, tag="work")
            for q in range(Q):
                first = (j * Q + q) * P
                nc.tensor.transpose(flipped_x[:, q, :], x_words[:, first : first + P], ident_f32[:])
            copy(out=grouped_words[:, j], in_=flipped_x[:].rearrange("p (g u) r -> p g r u", u=2))

        def transpose_unit(i):
            for j in range(UNIT_TILES):
                transpose_tile(i, j, scalar_copy)

        def quantise_tiles(i, first, count):
            if first == 0:
                x_codes = codes_pool.tile([P, UNIT_TILES * PASSES * P], U32, align_bytes=64, tag="x_codes")
                x_scales = codes_pool.tile([P, UNIT_TILES * PASSES * P], U8, align_bytes=64, tag="x_scales")
                code_tiles[i] = (x_codes, x_scales)
            x_codes, x_scales = code_tiles[i]
            words = slice(first * PASSES * P, (first + count) * PASSES * P)
            values = slice(first * IN, (first + count) * IN)
            nc.vector.quantize_mx(out=x_codes[:, words].bitcast(FP8X4), scales=x_scales[:, words], in_=grouped_tiles[i][:, values])

        def quantise_unit(i):
            quantise_tiles(i, 0, UNIT_TILES)

        results = {}

        def multiply_tiles(i, first, count, copy, pool=psum_acc, tag="acc"):
            b, h = divmod(i, UNITS_PER_EXAMPLE)
            x_codes, x_scales = code_tiles[i]
            acc = pool.tile([P, count, R], F32, tag=tag)
            for j in range(first, first + count):
                for g in range(PASSES):
                    x_cols = slice((j * PASSES + g) * P, (j * PASSES + g + 1) * P)
                    a_cols = slice((g * B + b) * R, (g * B + b + 1) * R)
                    nc.tensor.matmul_mx(
                        out=acc[:, j - first, :],
                        lhsT=x_codes[:, x_cols].bitcast(FP8X4),
                        lhsT_scale=x_scales[:, x_cols],
                        rhs=a_codes[:, a_cols].bitcast(FP8X4),
                        rhs_scale=a_scales[:, a_cols],
                        start=(g == 0),
                        stop=(g == PASSES - 1),
                    )
            if h == 0 and first == 0:
                result = out_pool.tile([P, UNITS_PER_EXAMPLE * UNIT_TILES * R], F32, tag="whole")
                results[b] = result
            start = h * UNIT_TILES + first
            copy(out=results[b][:, start * R : (start + count) * R], in_=acc[:].rearrange("p j r -> p (j r)"))
            if first + count == UNIT_TILES and (h == UNITS_PER_EXAMPLE - 1 or b == B - 1):
                cols = slice(h * UNIT_TILES * R if b == B - 1 else 0, (h + 1) * UNIT_TILES * R)
                nc.sync.dma_start(out=out_rows[b][:, cols], in_=results[b][:, cols])

        def multiply_unit(i, copy):
            multiply_tiles(i, 0, UNIT_TILES, copy)

        turn_weights()
        regroup_split(0)
        regroup_split(1)
        spread_weights()
        flip_split(0, (scalar_copy, scalar_copy))
        mix_on_vector(3)
        flip_split(1, (scalar_copy, scalar_copy))
        mix_on_vector(4)
        mix_bank(0, 0, vector_copy)
        mix_on_vector(1)
        transpose_tile(0, 0, scalar_copy)
        transpose_tile(0, 1, scalar_copy)
        regroup_split(2)
        mix_bank(0, 1, vector_copy)
        mix_on_vector(1)
        mix_bank(0, 2, vector_copy)
        mix_on_vector(1)
        transpose_tile(0, 2, scalar_copy)
        transpose_tile(0, 3, scalar_copy)
        load_unit(X_BUFS)
        regroup_split(3)
        mix_on_vector(1)
        flip_split(2, (scalar_copy, scalar_copy))
        mix_on_vector(1)
        mix_bank(0, 3, vector_copy)
        mix_on_vector(1)
        flip_split(3, (scalar_copy, scalar_copy))
        mix_on_vector(1)
        transpose_tile(1, 0, scalar_copy)
        transpose_tile(1, 1, scalar_copy)
        transpose_tile(1, 2, scalar_copy)
        transpose_tile(1, 3, scalar_copy)
        load_unit(1 + X_BUFS)
        quantise_unit(0)
        mix_bank(1, 0, vector_copy)
        mix_on_vector(1)
        mix_bank(1, 1, vector_copy)
        mix_on_vector(1)
        transpose_tile(2, 0, scalar_copy)
        transpose_tile(2, 1, scalar_copy)
        quantise_a(0, 0, 4)
        mix_bank(1, 2, vector_copy)
        mix_bank(1, 3, vector_copy)
        transpose_tile(2, 2, scalar_copy)
        transpose_tile(2, 3, scalar_copy)
        load_unit(2 + X_BUFS)
        quantise_unit(1)
        mix_on_vector(2)
        quantise_a(1, 0, 4)
        quantise_a(0, 4, 2)
        quantise_a(1, 4, 2)

        for i in range(3, 13, 2):
            for unit in (i, i + 1):
                transpose_unit(unit)
                if unit + X_BUFS < N_UNITS:
                    load_unit(unit + X_BUFS)
            for unit in (i - 1, i):
                mix_on_vector(4)
                quantise_unit(unit)
            if i == 11:
                mix_on_vector(len(terms))
                round_vector_mix()
                for g in range(PASSES):
                    quantise_a(g, 6, 2)
            for unit in (i - 3, i - 2):
                multiply_unit(unit, vector_copy if unit % 4 == 3 else scalar_copy)
        for i in range(13, N_UNITS):
            transpose_tile(i, 0, scalar_copy)
            transpose_tile(i, 1, vector_copy)
            transpose_tile(i, 2, scalar_copy)
            multiply_unit(i - 3, scalar_copy)
            transpose_tile(i, 3, scalar_copy)
            quantise_unit(i - 1)
        multiply_unit(N_UNITS - 3, scalar_copy)
        last = N_UNITS - 1
        for j in range(UNIT_TILES):
            quantise_tiles(last, j, 1)
        multiply_unit(last - 1, vector_copy)
        multiply_tiles(last, 0, 2, scalar_copy)
        multiply_tiles(last, 2, 2, scalar_copy, psum_work, "work")
